import numpy as np
import ml_dtypes


def mxq(x, axis, fmt="e4m3"):
    dtype, down = {"e4m3": (ml_dtypes.float8_e4m3fn, 7), "e5m2": (ml_dtypes.float8_e5m2, 14)}[fmt]
    v = np.moveaxis(np.asarray(x, np.float32).astype(ml_dtypes.bfloat16).astype(np.float64), axis, -1)
    blocks = v.reshape(v.shape[:-1] + (-1, 32))
    amax = np.abs(blocks).max(-1, keepdims=True)
    byte = np.maximum(np.where(amax > 0, np.frexp(amax)[1] - 1 + 127, 0) - down, 1)
    scale = np.exp2(byte - 127.0)
    codes = (blocks / scale).astype(np.float32).astype(dtype).astype(np.float64)
    return np.moveaxis((codes * scale).reshape(v.shape), -1, axis)


WIDE = False


def mx_kscale(k):
    if not WIDE:
        return np.ones(k)
    levels = np.array([10, -10, 5, -5, 0])
    a = np.random.permutation(np.resize(levels, k // 512 * 4)).reshape(k // 512, 4)
    idx = np.arange(k)
    return np.exp2(a[idx // 512, idx % 128 // 32])


BF16 = ml_dtypes.bfloat16


def bf(x):
    return np.asarray(x, np.float32).astype(BF16)


def f64(x):
    return np.asarray(x).astype(np.float64)


T, B, E, CDIM, H, K = 512, 4, 1024, 1024, 16, 32
R = CDIM // H
EPS = 1e-5


def layer_norm(v, g, b):
    m = v.mean(-1, keepdims=True)
    var = ((v - m) ** 2).mean(-1, keepdims=True)
    return (v - m) * (1.0 / np.sqrt(var + EPS)) * g + b


def setup_inputs():
    s = mx_kscale(CDIM)
    return {"h": bf(np.random.standard_normal((T, B, CDIM)) * s),
            "x": bf(np.random.standard_normal((T, B, E))),
            "ww": bf(np.random.standard_normal((H * K, CDIM)) / np.sqrt(CDIM) / s),
            "bw": bf(np.random.standard_normal(H * K) * 0.5),
            "w2": bf(np.random.standard_normal((E, CDIM)) * 3.0 / np.sqrt(CDIM) / s),
            "b2": bf(np.random.standard_normal(E) * 0.2),
            "gamma": bf(1.0 + 0.1 * np.random.standard_normal(E)),
            "beta": bf(np.random.standard_normal(E) * 0.2)}


def reference(h, x, ww, bw, w2, b2, gamma, beta):
    h = f64(h)
    z = ((mxq(h, 2, "e4m3") @ mxq(f64(ww).T, 0, "e4m3")) + f64(bw)).reshape(T, B, H, K)
    e = np.exp(z - z.max(-1, keepdims=True))
    w = e / e.sum(-1, keepdims=True)
    hp = np.concatenate([np.zeros((K - 1, B, H, R)), h.reshape(T, B, H, R)], 0)
    acc = np.zeros((T, B, H, R))
    for k in range(K):
        acc = acc + w[:, :, :, k:k + 1] * hp[k:k + T]
    c = acc.reshape(T, B, CDIM)
    y = (mxq(c, 2, "e4m3") @ mxq(f64(w2).T, 0, "e4m3")) + f64(b2)
    return layer_norm(f64(x) + y, f64(gamma), f64(beta))

@@ -1,0 +1,260 @@
+from contextlib import ExitStack
+
+import concourse.bass as bass
+import concourse.mybir as mybir
+import concourse.tile as tile
+from concourse.masks import make_identity
+
+FLOPS = 6576668672
+F32 = mybir.dt.float32
+BF16 = mybir.dt.bfloat16
+U32 = mybir.dt.uint32
+U8 = mybir.dt.uint8
+FP8X4 = mybir.dt.float8_e4m3fn_x4
+ALU = mybir.AluOpType
+ACT = mybir.ActivationFunctionType
+AX = mybir.AxisListType
+
+P = 128
+NB = 4
+NI = 4
+C = 1024
+H = 16
+K = 32
+R = 64
+CH = 63
+EPS = 1e-5
+
+
+def tile_dynamicconvdecoderlayer_pa_kernel(tc, h, x, ww, bw, w2, b2, gamma, beta, out):
+    nc = tc.nc
+    with ExitStack() as ctx:
+        const = ctx.enter_context(tc.tile_pool(name="const", bufs=1))
+        wst = ctx.enter_context(tc.tile_pool(name="wst", bufs=2))
+        hp = ctx.enter_context(tc.tile_pool(name="hp", bufs=2))
+        hfp = ctx.enter_context(tc.tile_pool(name="hfp", bufs=6))
+        sm = ctx.enter_context(tc.tile_pool(name="sm", bufs=2))
+        bp = ctx.enter_context(tc.tile_pool(name="bp", bufs=2))
+        cp = ctx.enter_context(tc.tile_pool(name="cp", bufs=2))
+        lp = ctx.enter_context(tc.tile_pool(name="lp", bufs=2))
+        ps_t = ctx.enter_context(tc.psum_pool(name="ps_t", bufs=2))
+        ps_z = ctx.enter_context(tc.psum_pool(name="ps_z", bufs=1))
+        ps_c = ctx.enter_context(tc.psum_pool(name="ps_c", bufs=2))
+        ps_k = ctx.enter_context(tc.psum_pool(name="ps_k", bufs=1))
+        ps_y = ctx.enter_context(tc.psum_pool(name="ps_y", bufs=2))
+
+        flat = out.rearrange("t b e -> (t b e)")
+
+        idf = const.tile([P, 2 * P], F32, name="idf")
+        make_identity(nc, idf[:, 0:P])
+        nc.vector.tensor_copy(out=idf[:, P:2 * P], in_=idf[:, 0:P])
+        idb = const.tile([P, 2 * P], BF16, name="idb")
+        nc.vector.tensor_copy(out=idb[:], in_=idf[:])
+        msk = const.tile([P, 4], F32, name="msk")
+        nc.vector.tensor_reduce(out=msk[:], in_=idf[:, 0:P].rearrange("p (j c) -> p j c", c=32), axis=AX.X, op=ALU.add)
+        nhalf = const.tile([P, 1], F32, name="nhalf")
+        nc.vector.memset(nhalf[:], -0.5)
+        bw_bc = const.tile([P, H * K], BF16, name="bw_bc")
+        nc.sync.dma_start(out=bw_bc[:], in_=bw.partition_broadcast(P))
+
+        stages = []
+        bands = []
+        corners = []
+        for i in range(3):
+            st = const.tile([P, 1024], F32, name="stage%d" % i)
+            nc.vector.memset(st[:], 0.0)
+            stages.append(st)
+        for i in range(NB):
+            bt = const.tile([P, H, P], F32, name="band%d" % i)
+            nc.gpsimd.memset(bt[:], 0.0)
+            bands.append(bt)
+            ct = const.tile([P, 4, P], F32, name="corner%d" % i)
+            nc.gpsimd.memset(ct[:], 0.0)
+            corners.append(ct)
+
+        wwq = const.tile([P, 2, 512], U32, name="wwq", align_bytes=64)
+        wws = const.tile([P, 2, 512], U8, name="wws", align_bytes=64)
+        w2q = const.tile([P, 2, 1024], U32, name="w2q", align_bytes=64)
+        w2s = const.tile([P, 2, 1024], U8, name="w2s", align_bytes=64)
+
+        gww = const.tile([P, 4096], BF16, name="gww", align_bytes=64)
+        gww32 = gww[:].bitcast(F32).rearrange("p (g c u) -> p g c u", g=2, u=2)
+        for rt in range(4):
+            raw = wst.tile([P, C], BF16, name="raw", tag="raw")
+            nc.sync.dma_start(out=raw[:], in_=ww[P * rt:P * rt + P, :])
+            tp = ps_t.tile([P, 4, P], F32, name="tp", tag="tp")
+            for gu in range(4):
+                nc.tensor.transpose(tp[:, gu, :], raw[:].bitcast(F32)[:, P * gu:P * gu + P], idf[:, 0:P])
+            nc.vector.tensor_copy(out=gww32[:, :, P * rt:P * rt + P, :], in_=tp[:].rearrange("p (g u) r -> p g r u", g=2))
+        for g in range(2):
+            nc.vector.quantize_mx(out=wwq[:, g, :].bitcast(FP8X4), scales=wws[:, g, :], in_=gww[:, 2048 * g:2048 * g + 2048])
+
+        hfs = {}
+
+        def phase1(ib, b):
+            tau = ib * NB + b
+            hb = hp.tile([P, C], BF16, name="hb", tag="hb")
+            nc.sync.dma_start(out=hb[:], in_=h[P * ib:P * ib + P, b, :])
+            tp = ps_t.tile([P, 4, P], F32, name="tp", tag="tp")
+            for gu in range(4):
+                nc.tensor.transpose(tp[:, gu, :], hb[:].bitcast(F32)[:, P * gu:P * gu + P], idf[:, 0:P])
+            hg = hp.tile([P, C], BF16, name="hg", tag="hg", align_bytes=64)
+            nc.scalar.copy(out=hg[:].bitcast(F32).rearrange("p (g r u) -> p g r u", g=2, u=2),
+                           in_=tp[:].rearrange("p (g u) r -> p g r u", g=2))
+            hq = hp.tile([P, 256], U32, name="hq", tag="hq", align_bytes=64)
+            hs = hp.tile([P, 256], U8, name="hs", tag="hs", align_bytes=64)
+            nc.vector.quantize_mx(out=hq[:].bitcast(FP8X4), scales=hs[:], in_=hg[:])
+            z = ps_z.tile([P, 512], F32, name="z", tag="z")
+            for g in range(2):
+                nc.tensor.matmul_mx(out=z[:], lhsT=hq[:, P * g:P * g + P].bitcast(FP8X4), lhsT_scale=hs[:, P * g:P * g + P],
+                                    rhs=wwq[:, g, :].bitcast(FP8X4), rhs_scale=wws[:, g, :], start=(g == 0), stop=(g == 1))
+            hf = hfp.tile([P, C], F32, name="hf", tag="hf")
+            nc.gpsimd.tensor_scalar(out=hf[:], in0=hb[:], scalar1=1.0, scalar2=0.0, op0=ALU.mult, op1=ALU.add)
+            hfs[tau] = hf
+            zb = sm.tile([P, H, K], F32, name="zb", tag="zb")
+            nc.vector.tensor_tensor(out=zb[:].rearrange("p n k -> p (n k)"), in0=z[:], in1=bw_bc[:], op=ALU.add)
+            mx = sm.tile([P, H], F32, name="mx", tag="mx")
+            nc.vector.tensor_reduce(out=mx[:], in_=zb[:], axis=AX.X, op=ALU.max)
+            nc.vector.tensor_tensor(out=zb[:], in0=zb[:], in1=mx[:].unsqueeze(2).to_broadcast([P, H, K]), op=ALU.subtract)
+            ex = sm.tile([P, H, K], F32, name="ex", tag="ex")
+            nc.scalar.activation(out=ex[:], in_=zb[:], func=ACT.Exp)
+            sums = sm.tile([P, H], F32, name="sums", tag="sums")
+            nc.vector.tensor_reduce(out=sums[:], in_=ex[:], axis=AX.X, op=ALU.add)
+            rs = sm.tile([P, H], F32, name="rs", tag="rs")
+            nc.vector.reciprocal(out=rs[:], in_=sums[:])
+            st = stages[tau % 3]
+            sv = st[:, 0:H * CH].rearrange("p (n c) -> p n c", c=CH)
+            nc.vector.tensor_tensor(out=sv[:, :, 0:K], in0=ex[:], in1=rs[:].unsqueeze(2).to_broadcast([P, H, K]), op=ALU.mult)
+            nc.sync.dma_start(out=flat[tau * 131072:(tau + 1) * 131072].rearrange("(p w) -> p w", w=1024), in_=st[:])
+
+        def read_bands(ib, b):
+            tau = ib * NB + b
+            for a in range(4):
+                base = tau * 131072 + a * 32 * 1024
+                src = flat[base:base + 32 * 1023].rearrange("(i w) -> i w", w=1023)[:, 0:H * CH].rearrange("i (n c) -> i n c", c=CH)
+                if a == 0:
+                    nc.sync.dma_start(out=bands[b][0:32, :, 0:32], in_=src[:, :, 31:63])
+                    if ib > 0:
+                        for j in range(4):
+                            nc.sync.dma_start(out=corners[b][32 * j:32 * j + 32, :, 32 * j + 1:32 * j + 32], in_=src[:, 4 * j:4 * j + 4, 0:31])
+                else:
+                    nc.sync.dma_start(out=bands[b][32 * a:32 * a + 32, :, 32 * (a - 1) + 1:32 * (a - 1) + 64], in_=src[:, :, 0:63])
+
+        lts = {}
+
+        def phase2a(ib, b):
+            lt = bp.tile([P, H, P], F32, name="lt", tag="lt")
+            for j in range(4):
+                off = (P - 32 * j) % P
+                tp = ps_t.tile([P, 4, P], F32, name="tp", tag="tp")
+                for q in range(4):
+                    nc.tensor.transpose(tp[:, q, :], bands[b][:, 4 * j + q, :], idf[:, off:off + P])
+                if j % 2 == 0:
+                    nc.scalar.copy(out=lt[:, 4 * j:4 * j + 4, :], in_=tp[:])
+                else:
+                    nc.vector.tensor_copy(out=lt[:, 4 * j:4 * j + 4, :], in_=tp[:])
+            lc = None
+            if ib > 0:
+                lc = bp.tile([P, 4, P], F32, name="lc", tag="lc")
+                tp = ps_t.tile([P, 4, P], F32, name="tp", tag="tp")
+                for q in range(4):
+                    nc.tensor.transpose(tp[:, q, :], corners[b][:, q, :], idf[:, 0:P])
+                nc.scalar.copy(out=lc[:], in_=tp[:])
+            lts[(ib, b)] = (lt, lc)
+
+        def phase2b(ib, b):
+            tau = ib * NB + b
+            lt, lc = lts[(ib, b)]
+            hf = hfs[tau]
+            cps = []
+            for half in range(2):
+                cd = ps_c.tile([P, 512], F32, name="cd", tag="cd")
+                for m in range(8):
+                    n = 8 * half + m
+                    nc.tensor.matmul(out=cd[:, R * m:R * m + R], lhsT=lt[:, n, :], rhs=hf[:, R * n:R * n + R], start=True, stop=True)
+                cps.append(cd)
+            cb = cp.tile([P, C], BF16, name="cb", tag="cb")
+            if ib == 0:
+                nc.scalar.copy(out=cb[:, 0:512], in_=cps[0][:])
+                nc.scalar.copy(out=cb[:, 512:1024], in_=cps[1][:])
+            else:
+                hcb = cp.tile([P, 256], BF16, name="hcb", tag="hcb")
+                for j in range(4):
+                    nc.sync.dma_start(out=hcb[32 * j:32 * j + 32, :], in_=h[P * ib - 32:P * ib, b, 256 * j:256 * j + 256])
+                hcf = cp.tile([P, 256], F32, name="hcf", tag="hcf")
+                nc.gpsimd.tensor_scalar(out=hcf[:], in0=hcb[:], scalar1=1.0, scalar2=0.0, op0=ALU.mult, op1=ALU.add)
+                yk = ps_k.tile([P, 256], F32, name="yk", tag="yk")
+                for q in range(4):
+                    nc.tensor.matmul(out=yk[:, R * q:R * q + R], lhsT=lc[:, q, :], rhs=hcf[:, R * q:R * q + R], start=True, stop=True)
+                ysb = cp.tile([P, 256], F32, name="ysb", tag="ysb")
+                nc.scalar.copy(out=ysb[:], in_=yk[:])
+                for j in range(4):
+                    nc.vector.scalar_tensor_tensor(out=cb[:, 256 * j:256 * j + 256], in0=ysb[:], scalar=msk[:, j:j + 1],
+                                                   in1=cps[j // 2][:, 256 * (j % 2):256 * (j % 2) + 256], op0=ALU.mult, op1=ALU.add)
+            tpb = ps_t.tile([P, 8, P], BF16, name="tpb", tag="tp")
+            for ch in range(8):
+                j = ch // 2
+                nc.tensor.transpose(tpb[:, ch, :], cb[:, P * ch:P * ch + P], idb[:, 32 * j:32 * j + P])
+            cg = cp.tile([P, C], BF16, name="cg", tag="cg", align_bytes=64)
+            nc.scalar.copy(out=cg[:].rearrange("p (g r t) -> p g r t", g=2, t=4), in_=tpb[:].rearrange("p (g t) r -> p g r t", g=2))
+            cq = cp.tile([P, 256], U32, name="cq", tag="cq", align_bytes=64)
+            cs = cp.tile([P, 256], U8, name="cs", tag="cs", align_bytes=64)
+            nc.vector.quantize_mx(out=cq[:].bitcast(FP8X4), scales=cs[:], in_=cg[:])
+            xt = lp.tile([P, C], BF16, name="xt", tag="xt")
+            nc.sync.dma_start(out=xt[:], in_=x[P * ib:P * ib + P, b, :])
+            xb = lp.tile([P, C], F32, name="xb", tag="xb")
+            nc.gpsimd.tensor_tensor(out=xb[:], in0=xt[:], in1=b2_bc[:], op=ALU.add)
+            v = lp.tile([P, C], F32, name="v", tag="v")
+            s2 = lp.tile([P, 2], F32, name="s2", tag="s2")
+            for e2 in range(2):
+                yp = ps_y.tile([P, 512], F32, name="yp", tag="yp")
+                for g in range(2):
+                    nc.tensor.matmul_mx(out=yp[:], lhsT=cq[:, P * g:P * g + P].bitcast(FP8X4), lhsT_scale=cs[:, P * g:P * g + P],
+                                        rhs=w2q[:, g, 512 * e2:512 * e2 + 512].bitcast(FP8X4), rhs_scale=w2s[:, g, 512 * e2:512 * e2 + 512],
+                                        start=(g == 0), stop=(g == 1))
+                nc.vector.scalar_tensor_tensor(out=v[:, 512 * e2:512 * e2 + 512], in0=yp[:], scalar=1.0, in1=xb[:, 512 * e2:512 * e2 + 512],
+                                               op0=ALU.mult, op1=ALU.add, accum_out=s2[:, e2:e2 + 1])
+            nm = lp.tile([P, 1], F32, name="nm", tag="nm")
+            nc.vector.tensor_scalar(out=nm[:], in0=s2[:, 0:1], scalar1=s2[:, 1:2], scalar2=-1.0 / C, op0=ALU.add, op1=ALU.mult)
+            junk = lp.tile([P, C], BF16, name="junk", tag="junk")
+            ss = lp.tile([P, 1], F32, name="ss", tag="ss")
+            nc.scalar.activation(out=junk[:], in_=v[:], func=ACT.Square, bias=nm[:], scale=1.0, accum_out=ss[:])
+            ve = lp.tile([P, 1], F32, name="ve", tag="ve")
+            nc.gpsimd.tensor_scalar(out=ve[:], in0=ss[:], scalar1=1.0 / C, scalar2=EPS, op0=ALU.mult, op1=ALU.add)
+            rstd = lp.tile([P, 1], F32, name="rstd", tag="rstd")
+            nc.gpsimd.tensor_tensor(out=rstd[:], in0=ve[:], in1=nhalf[:], op=ALU.pow)
+            t1 = lp.tile([P, C], F32, name="t1", tag="t1")
+            nc.vector.scalar_tensor_tensor(out=t1[:], in0=v[:], scalar=nm[:], in1=g_bc[:], op0=ALU.add, op1=ALU.mult)
+            nc.vector.scalar_tensor_tensor(out=t1[:], in0=t1[:], scalar=rstd[:], in1=be_bc[:], op0=ALU.mult, op1=ALU.add)
+            nc.sync.dma_start(out=out[P * ib:P * ib + P, b, :], in_=t1[:])
+
+        for b in range(NB):
+            phase1(0, b)
+            read_bands(0, b)
+
+        b2_bc = const.tile([P, C], BF16, name="b2_bc")
+        nc.sync.dma_start(out=b2_bc[:], in_=b2.partition_broadcast(P))
+        g_bc = const.tile([P, C], BF16, name="g_bc")
+        nc.sync.dma_start(out=g_bc[:], in_=gamma.partition_broadcast(P))
+        be_bc = const.tile([P, C], BF16, name="be_bc")
+        nc.sync.dma_start(out=be_bc[:], in_=beta.partition_broadcast(P))
+        gw2 = const.tile([P, 8192], BF16, name="gw2", align_bytes=64)
+        gw2v = gw2[:].rearrange("p (g c t) -> p g c t", g=2, t=4)
+        for rt in range(8):
+            raw = wst.tile([P, C], BF16, name="raw", tag="raw")
+            nc.sync.dma_start(out=raw[:], in_=w2[P * rt:P * rt + P, :])
+            tpb = ps_t.tile([P, 8, P], BF16, name="tpb", tag="tp")
+            for gt in range(8):
+                nc.tensor.transpose(tpb[:, gt, :], raw[:, P * gt:P * gt + P], idb[:, 0:P])
+            nc.vector.tensor_copy(out=gw2v[:, :, P * rt:P * rt + P, :], in_=tpb[:].rearrange("p (g t) r -> p g r t", g=2))
+        for g in range(2):
+            nc.vector.quantize_mx(out=w2q[:, g, :].bitcast(FP8X4), scales=w2s[:, g, :], in_=gw2[:, 4096 * g:4096 * g + 4096])
+
+        for ib in range(NI):
+            for b in range(NB):
+                if ib + 1 < NI:
+                    phase1(ib + 1, b)
+                phase2a(ib, b)
+                if ib + 1 < NI:
+                    read_bands(ib + 1, b)
+                phase2b(ib, b)

@@ -1,8 +1,6 @@
 from contextlib import ExitStack
 
-import concourse.bass as bass
 import concourse.mybir as mybir
-import concourse.tile as tile
 from concourse.masks import make_identity
 
 FLOPS = 6576668672
@@ -18,12 +16,15 @@ AX = mybir.AxisListType
 P = 128
 NB = 4
 NI = 4
+NT = NB * NI
 C = 1024
 H = 16
 K = 32
 R = 64
 CH = 63
 EPS = 1e-5
+NBAND = 3
+PINNED = True
 
 
 def tile_dynamicconvdecoderlayer_pa_kernel(tc, h, x, ww, bw, w2, b2, gamma, beta, out):
@@ -31,19 +32,22 @@ def tile_dynamicconvdecoderlayer_pa_kernel(tc, h, x, ww, bw, w2, b2, gamma, beta
     with ExitStack() as ctx:
         const = ctx.enter_context(tc.tile_pool(name="const", bufs=1))
         wst = ctx.enter_context(tc.tile_pool(name="wst", bufs=2))
-        hp = ctx.enter_context(tc.tile_pool(name="hp", bufs=2))
-        hfp = ctx.enter_context(tc.tile_pool(name="hfp", bufs=6))
-        sm = ctx.enter_context(tc.tile_pool(name="sm", bufs=2))
-        bp = ctx.enter_context(tc.tile_pool(name="bp", bufs=2))
-        cp = ctx.enter_context(tc.tile_pool(name="cp", bufs=2))
-        lp = ctx.enter_context(tc.tile_pool(name="lp", bufs=2))
-        ps_t = ctx.enter_context(tc.psum_pool(name="ps_t", bufs=2))
+        p2 = ctx.enter_context(tc.tile_pool(name="p2", bufs=2))
+        p3 = ctx.enter_context(tc.tile_pool(name="p3", bufs=3))
+        hfp = ctx.enter_context(tc.tile_pool(name="hfp", bufs=7))
+        p1 = ctx.enter_context(tc.tile_pool(name="p1", bufs=1))
+        ps_t = ctx.enter_context(tc.psum_pool(name="ps_t", bufs=3))
         ps_z = ctx.enter_context(tc.psum_pool(name="ps_z", bufs=1))
         ps_c = ctx.enter_context(tc.psum_pool(name="ps_c", bufs=2))
-        ps_k = ctx.enter_context(tc.psum_pool(name="ps_k", bufs=1))
         ps_y = ctx.enter_context(tc.psum_pool(name="ps_y", bufs=2))
+        if PINNED:
+            ctx.enter_context(tc.manual_schedule())
 
         flat = out.rearrange("t b e -> (t b e)")
+        T = {}
+
+        def ok(t):
+            return 0 <= t < NT
 
         idf = const.tile([P, 2 * P], F32, name="idf")
         make_identity(nc, idf[:, 0:P])
@@ -55,206 +59,399 @@ def tile_dynamicconvdecoderlayer_pa_kernel(tc, h, x, ww, bw, w2, b2, gamma, beta
         nhalf = const.tile([P, 1], F32, name="nhalf")
         nc.vector.memset(nhalf[:], -0.5)
         bw_bc = const.tile([P, H * K], BF16, name="bw_bc")
-        nc.sync.dma_start(out=bw_bc[:], in_=bw.partition_broadcast(P))
-
-        stages = []
-        bands = []
-        corners = []
-        for i in range(3):
-            st = const.tile([P, 1024], F32, name="stage%d" % i)
-            nc.vector.memset(st[:], 0.0)
-            stages.append(st)
-        for i in range(NB):
-            bt = const.tile([P, H, P], F32, name="band%d" % i)
-            nc.gpsimd.memset(bt[:], 0.0)
-            bands.append(bt)
-            ct = const.tile([P, 4, P], F32, name="corner%d" % i)
-            nc.gpsimd.memset(ct[:], 0.0)
-            corners.append(ct)
-
+        b2_bc = const.tile([P, C], BF16, name="b2_bc")
+        g_bc = const.tile([P, C], BF16, name="g_bc")
+        be_bc = const.tile([P, C], BF16, name="be_bc")
         wwq = const.tile([P, 2, 512], U32, name="wwq", align_bytes=64)
         wws = const.tile([P, 2, 512], U8, name="wws", align_bytes=64)
         w2q = const.tile([P, 2, 1024], U32, name="w2q", align_bytes=64)
         w2s = const.tile([P, 2, 1024], U8, name="w2s", align_bytes=64)
-
         gww = const.tile([P, 4096], BF16, name="gww", align_bytes=64)
         gww32 = gww[:].bitcast(F32).rearrange("p (g c u) -> p g c u", g=2, u=2)
+        gw2 = const.tile([P, 8192], BF16, name="gw2", align_bytes=64)
+        gw2v = gw2[:].rearrange("p (g c t) -> p g c t", g=2, t=4)
+        stages = [const.tile([P, 1024], F32, name="stage%d" % i) for i in range(3)]
+        bands = [const.tile([P, H, P], F32, name="band%d" % i) for i in range(NBAND)]
+        corners = [const.tile([P, 4, P], F32, name="corner%d" % i) for i in range(NBAND)]
+
+        def ld(t):
+            if not ok(t):
+                return
+            hb = p3.tile([P, C], BF16, name="hb", tag="hb")
+            nc.sync.dma_start(out=hb[:], in_=h[P * (t // NB):P * (t // NB) + P, t % NB, :])
+            T[("hb", t)] = hb
+
+        def ld_x(t):
+            if not ok(t):
+                return
+            xt = p3.tile([P, C], BF16, name="xt", tag="xt")
+            nc.sync.dma_start(out=xt[:], in_=x[P * (t // NB):P * (t // NB) + P, t % NB, :])
+            T[("xt", t)] = xt
+
+        def ld_hc(ib):
+            hcb = p2.tile([P, NB, 256], BF16, name="hcb", tag="hcb")
+            for j in range(4):
+                nc.sync.dma_start(out=hcb[32 * j:32 * j + 32, :, :], in_=h[P * ib - 32:P * ib, :, 256 * j:256 * j + 256])
+            T[("hcb", ib)] = hcb
+
+        raws = []
         for rt in range(4):
-            raw = wst.tile([P, C], BF16, name="raw", tag="raw")
+            raw = p1.tile([P, C], BF16, name="rawww%d" % rt)
             nc.sync.dma_start(out=raw[:], in_=ww[P * rt:P * rt + P, :])
+            raws.append(raw)
+        ld(0)
+        nc.sync.dma_start(out=bw_bc[:], in_=bw.partition_broadcast(P))
+        for st in stages:
+            nc.vector.memset(st[:], 0.0)
+        for rt in range(4):
             tp = ps_t.tile([P, 4, P], F32, name="tp", tag="tp")
             for gu in range(4):
-                nc.tensor.transpose(tp[:, gu, :], raw[:].bitcast(F32)[:, P * gu:P * gu + P], idf[:, 0:P])
-            nc.vector.tensor_copy(out=gww32[:, :, P * rt:P * rt + P, :], in_=tp[:].rearrange("p (g u) r -> p g r u", g=2))
+                nc.tensor.transpose(tp[:, gu, :], raws[rt][:].bitcast(F32)[:, P * gu:P * gu + P], idf[:, 0:P])
+            if rt % 2 == 0:
+                nc.vector.tensor_copy(out=gww32[:, :, P * rt:P * rt + P, :], in_=tp[:].rearrange("p (g u) r -> p g r u", g=2))
+            else:
+                nc.scalar.copy(out=gww32[:, :, P * rt:P * rt + P, :], in_=tp[:].rearrange("p (g u) r -> p g r u", g=2))
         for g in range(2):
             nc.vector.quantize_mx(out=wwq[:, g, :].bitcast(FP8X4), scales=wws[:, g, :], in_=gww[:, 2048 * g:2048 * g + 2048])
+        for i in range(NBAND):
+            nc.vector.memset(bands[i][:], 0.0)
+            nc.vector.memset(corners[i][:], 0.0)
 
-        hfs = {}
-
-        def phase1(ib, b):
-            tau = ib * NB + b
-            hb = hp.tile([P, C], BF16, name="hb", tag="hb")
-            nc.sync.dma_start(out=hb[:], in_=h[P * ib:P * ib + P, b, :])
+        def pe_hT(t):
+            if not ok(t):
+                return
             tp = ps_t.tile([P, 4, P], F32, name="tp", tag="tp")
+            hb = T[("hb", t)]
             for gu in range(4):
                 nc.tensor.transpose(tp[:, gu, :], hb[:].bitcast(F32)[:, P * gu:P * gu + P], idf[:, 0:P])
-            hg = hp.tile([P, C], BF16, name="hg", tag="hg", align_bytes=64)
+            T[("hT", t)] = tp
+
+        def act_hg(t):
+            if not ok(t):
+                return
+            hg = p2.tile([P, C], BF16, name="hg", tag="hg", align_bytes=64)
             nc.scalar.copy(out=hg[:].bitcast(F32).rearrange("p (g r u) -> p g r u", g=2, u=2),
-                           in_=tp[:].rearrange("p (g u) r -> p g r u", g=2))
-            hq = hp.tile([P, 256], U32, name="hq", tag="hq", align_bytes=64)
-            hs = hp.tile([P, 256], U8, name="hs", tag="hs", align_bytes=64)
-            nc.vector.quantize_mx(out=hq[:].bitcast(FP8X4), scales=hs[:], in_=hg[:])
+                           in_=T[("hT", t)][:].rearrange("p (g u) r -> p g r u", g=2))
+            T[("hg", t)] = hg
+
+        def pool_hf(t):
+            if not ok(t):
+                return
+            hf = hfp.tile([P, C], F32, name="hf", tag="hf")
+            nc.gpsimd.tensor_scalar(out=hf[:], in0=T[("hb", t)][:], scalar1=1.0, scalar2=0.0, op0=ALU.mult, op1=ALU.add)
+            T[("hf", t)] = hf
+
+        def dve_qh(t):
+            if not ok(t):
+                return
+            hq = p3.tile([P, 256], U32, name="hq", tag="hq", align_bytes=64)
+            hs = p3.tile([P, 256], U8, name="hs", tag="hs", align_bytes=64)
+            nc.vector.quantize_mx(out=hq[:].bitcast(FP8X4), scales=hs[:], in_=T[("hg", t)][:])
+            T[("hq", t)] = (hq, hs)
+
+        def pe_mm1(t):
+            if not ok(t):
+                return
+            hq, hs = T[("hq", t)]
             z = ps_z.tile([P, 512], F32, name="z", tag="z")
             for g in range(2):
                 nc.tensor.matmul_mx(out=z[:], lhsT=hq[:, P * g:P * g + P].bitcast(FP8X4), lhsT_scale=hs[:, P * g:P * g + P],
                                     rhs=wwq[:, g, :].bitcast(FP8X4), rhs_scale=wws[:, g, :], start=(g == 0), stop=(g == 1))
-            hf = hfp.tile([P, C], F32, name="hf", tag="hf")
-            nc.gpsimd.tensor_scalar(out=hf[:], in0=hb[:], scalar1=1.0, scalar2=0.0, op0=ALU.mult, op1=ALU.add)
-            hfs[tau] = hf
-            zb = sm.tile([P, H, K], F32, name="zb", tag="zb")
-            nc.vector.tensor_tensor(out=zb[:].rearrange("p n k -> p (n k)"), in0=z[:], in1=bw_bc[:], op=ALU.add)
-            mx = sm.tile([P, H], F32, name="mx", tag="mx")
+            T[("z", t)] = z
+
+        def dve_sm1(t):
+            if not ok(t):
+                return
+            zb = p2.tile([P, H, K], F32, name="zb", tag="zb")
+            nc.vector.tensor_tensor(out=zb[:].rearrange("p n k -> p (n k)"), in0=T[("z", t)][:], in1=bw_bc[:], op=ALU.add)
+            mx = p2.tile([P, H], F32, name="mx", tag="mx")
             nc.vector.tensor_reduce(out=mx[:], in_=zb[:], axis=AX.X, op=ALU.max)
             nc.vector.tensor_tensor(out=zb[:], in0=zb[:], in1=mx[:].unsqueeze(2).to_broadcast([P, H, K]), op=ALU.subtract)
-            ex = sm.tile([P, H, K], F32, name="ex", tag="ex")
-            nc.scalar.activation(out=ex[:], in_=zb[:], func=ACT.Exp)
-            sums = sm.tile([P, H], F32, name="sums", tag="sums")
-            nc.vector.tensor_reduce(out=sums[:], in_=ex[:], axis=AX.X, op=ALU.add)
-            rs = sm.tile([P, H], F32, name="rs", tag="rs")
-            nc.vector.reciprocal(out=rs[:], in_=sums[:])
-            st = stages[tau % 3]
-            sv = st[:, 0:H * CH].rearrange("p (n c) -> p n c", c=CH)
-            nc.vector.tensor_tensor(out=sv[:, :, 0:K], in0=ex[:], in1=rs[:].unsqueeze(2).to_broadcast([P, H, K]), op=ALU.mult)
-            nc.sync.dma_start(out=flat[tau * 131072:(tau + 1) * 131072].rearrange("(p w) -> p w", w=1024), in_=st[:])
+            T[("zb", t)] = zb
 
-        def read_bands(ib, b):
-            tau = ib * NB + b
+        def act_exp(t):
+            if not ok(t):
+                return
+            ex = p2.tile([P, H, K], F32, name="ex", tag="ex")
+            nc.scalar.activation(out=ex[:], in_=T[("zb", t)][:], func=ACT.Exp)
+            T[("ex", t)] = ex
+
+        def dve_sm2(t):
+            if not ok(t):
+                return
+            ex = T[("ex", t)]
+            sums = p2.tile([P, H], F32, name="sums", tag="sums")
+            nc.vector.tensor_reduce(out=sums[:], in_=ex[:], axis=AX.X, op=ALU.add)
+            rs = p2.tile([P, H], F32, name="rs", tag="rs")
+            nc.vector.reciprocal(out=rs[:], in_=sums[:])
+            sv = stages[t % 3][:, 0:H * CH].rearrange("p (n c) -> p n c", c=CH)
+            nc.vector.tensor_tensor(out=sv[:, :, 0:K], in0=ex[:], in1=rs[:].unsqueeze(2).to_broadcast([P, H, K]), op=ALU.mult)
+
+        def sp_write(t):
+            if not ok(t):
+                return
+            nc.sync.dma_start(out=flat[t * 131072:(t + 1) * 131072].rearrange("(p w) -> p w", w=1024), in_=stages[t % 3][:])
+
+        def sp_reads(t):
+            if not ok(t):
+                return
+            bt = bands[t % NBAND]
+            ct = corners[t % NBAND]
             for a in range(4):
-                base = tau * 131072 + a * 32 * 1024
+                base = t * 131072 + a * 32 * 1024
                 src = flat[base:base + 32 * 1023].rearrange("(i w) -> i w", w=1023)[:, 0:H * CH].rearrange("i (n c) -> i n c", c=CH)
                 if a == 0:
-                    nc.sync.dma_start(out=bands[b][0:32, :, 0:32], in_=src[:, :, 31:63])
-                    if ib > 0:
+                    if t >= NB:
                         for j in range(4):
-                            nc.sync.dma_start(out=corners[b][32 * j:32 * j + 32, :, 32 * j + 1:32 * j + 32], in_=src[:, 4 * j:4 * j + 4, 0:31])
+                            nc.sync.dma_start(out=ct[32 * j:32 * j + 32, :, 32 * j + 1:32 * j + 32], in_=src[:, 4 * j:4 * j + 4, 0:31])
+                    nc.sync.dma_start(out=bt[0:32, :, 0:32], in_=src[:, :, 31:63])
                 else:
-                    nc.sync.dma_start(out=bands[b][32 * a:32 * a + 32, :, 32 * (a - 1) + 1:32 * (a - 1) + 64], in_=src[:, :, 0:63])
+                    nc.sync.dma_start(out=bt[32 * a:32 * a + 32, :, 32 * (a - 1) + 1:32 * (a - 1) + 64], in_=src[:, :, 0:63])
 
-        lts = {}
+        def pe_cornerT(t):
+            if not ok(t) or t < NB:
+                return
+            tp = ps_t.tile([P, 4, P], F32, name="tp", tag="tp")
+            for q in range(4):
+                nc.tensor.transpose(tp[:, q, :], corners[t % NBAND][:, q, :], idf[:, 0:P])
+            T[("lcT", t)] = tp
 
-        def phase2a(ib, b):
-            lt = bp.tile([P, H, P], F32, name="lt", tag="lt")
-            for j in range(4):
-                off = (P - 32 * j) % P
-                tp = ps_t.tile([P, 4, P], F32, name="tp", tag="tp")
-                for q in range(4):
-                    nc.tensor.transpose(tp[:, q, :], bands[b][:, 4 * j + q, :], idf[:, off:off + P])
-                if j % 2 == 0:
-                    nc.scalar.copy(out=lt[:, 4 * j:4 * j + 4, :], in_=tp[:])
-                else:
-                    nc.vector.tensor_copy(out=lt[:, 4 * j:4 * j + 4, :], in_=tp[:])
-            lc = None
-            if ib > 0:
-                lc = bp.tile([P, 4, P], F32, name="lc", tag="lc")
-                tp = ps_t.tile([P, 4, P], F32, name="tp", tag="tp")
-                for q in range(4):
-                    nc.tensor.transpose(tp[:, q, :], corners[b][:, q, :], idf[:, 0:P])
-                nc.scalar.copy(out=lc[:], in_=tp[:])
-            lts[(ib, b)] = (lt, lc)
+        def act_lc(t):
+            if not ok(t) or t < NB:
+                return
+            lc = p2.tile([P, 4, P], F32, name="lc", tag="lc")
+            nc.scalar.copy(out=lc[:], in_=T[("lcT", t)][:])
+            T[("lc", t)] = lc
 
-        def phase2b(ib, b):
-            tau = ib * NB + b
-            lt, lc = lts[(ib, b)]
-            hf = hfs[tau]
-            cps = []
-            for half in range(2):
-                cd = ps_c.tile([P, 512], F32, name="cd", tag="cd")
-                for m in range(8):
-                    n = 8 * half + m
-                    nc.tensor.matmul(out=cd[:, R * m:R * m + R], lhsT=lt[:, n, :], rhs=hf[:, R * n:R * n + R], start=True, stop=True)
-                cps.append(cd)
-            cb = cp.tile([P, C], BF16, name="cb", tag="cb")
-            if ib == 0:
-                nc.scalar.copy(out=cb[:, 0:512], in_=cps[0][:])
-                nc.scalar.copy(out=cb[:, 512:1024], in_=cps[1][:])
+        def pool_hcf(t):
+            if not ok(t) or t < NB:
+                return
+            hcf = p2.tile([P, 256], F32, name="hcf", tag="hcf")
+            nc.gpsimd.tensor_scalar(out=hcf[:], in0=T[("hcb", t // NB)][:, t % NB, :], scalar1=1.0, scalar2=0.0, op0=ALU.mult, op1=ALU.add)
+            T[("hcf", t)] = hcf
+
+        def pe_cornermm(t):
+            if not ok(t) or t < NB:
+                return
+            yk = ps_t.tile([P, 256], F32, name="yk", tag="tp")
+            lc = T[("lc", t)]
+            hcf = T[("hcf", t)]
+            for q in range(4):
+                nc.tensor.matmul(out=yk[:, R * q:R * q + R], lhsT=lc[:, q, :], rhs=hcf[:, R * q:R * q + R], start=True, stop=True)
+            T[("yk", t)] = yk
+
+        def act_ysb(t):
+            if not ok(t) or t < NB:
+                return
+            ysb = p2.tile([P, 256], F32, name="ysb", tag="ysb")
+            nc.scalar.copy(out=ysb[:], in_=T[("yk", t)][:])
+            T[("ysb", t)] = ysb
+
+        def pe_bandT(t, j):
+            if not ok(t):
+                return
+            off = (P - 32 * j) % P
+            tp = ps_t.tile([P, 4, P], F32, name="tp", tag="tp")
+            for q in range(4):
+                nc.tensor.transpose(tp[:, q, :], bands[t % NBAND][:, 4 * j + q, :], idf[:, off:off + P])
+            T[("ltT", t, j)] = tp
+
+        def act_lt(t, j):
+            if not ok(t):
+                return
+            if j == 0:
+                T[("lt", t)] = p2.tile([P, H, P], F32, name="lt", tag="lt")
+            nc.scalar.copy(out=T[("lt", t)][:, 4 * j:4 * j + 4, :], in_=T[("ltT", t, j)][:])
+
+        def pe_mm(t, j):
+            if not ok(t):
+                return
+            if j % 2 == 0:
+                T[("cd", t, j // 2)] = ps_c.tile([P, 512], F32, name="cd", tag="cd")
+            cd = T[("cd", t, j // 2)]
+            lt = T[("lt", t)]
+            hf = T[("hf", t)]
+            for q in range(4):
+                n = 4 * j + q
+                m = n % 8
+                nc.tensor.matmul(out=cd[:, R * m:R * m + R], lhsT=lt[:, n, :], rhs=hf[:, R * n:R * n + R], start=True, stop=True)
+
+        def dve_c(t, half):
+            if not ok(t):
+                return
+            if half == 0:
+                T[("cb", t)] = p2.tile([P, C], BF16, name="cb", tag="cb")
+            cb = T[("cb", t)]
+            cd = T[("cd", t, half)]
+            if t < NB:
+                nc.vector.tensor_copy(out=cb[:, 512 * half:512 * half + 512], in_=cd[:])
             else:
-                hcb = cp.tile([P, 256], BF16, name="hcb", tag="hcb")
-                for j in range(4):
-                    nc.sync.dma_start(out=hcb[32 * j:32 * j + 32, :], in_=h[P * ib - 32:P * ib, b, 256 * j:256 * j + 256])
-                hcf = cp.tile([P, 256], F32, name="hcf", tag="hcf")
-                nc.gpsimd.tensor_scalar(out=hcf[:], in0=hcb[:], scalar1=1.0, scalar2=0.0, op0=ALU.mult, op1=ALU.add)
-                yk = ps_k.tile([P, 256], F32, name="yk", tag="yk")
-                for q in range(4):
-                    nc.tensor.matmul(out=yk[:, R * q:R * q + R], lhsT=lc[:, q, :], rhs=hcf[:, R * q:R * q + R], start=True, stop=True)
-                ysb = cp.tile([P, 256], F32, name="ysb", tag="ysb")
-                nc.scalar.copy(out=ysb[:], in_=yk[:])
-                for j in range(4):
-                    nc.vector.scalar_tensor_tensor(out=cb[:, 256 * j:256 * j + 256], in0=ysb[:], scalar=msk[:, j:j + 1],
-                                                   in1=cps[j // 2][:, 256 * (j % 2):256 * (j % 2) + 256], op0=ALU.mult, op1=ALU.add)
+                for j in (2 * half, 2 * half + 1):
+                    nc.vector.scalar_tensor_tensor(out=cb[:, 256 * j:256 * j + 256], in0=T[("ysb", t)][:], scalar=msk[:, j:j + 1],
+                                                   in1=cd[:, 256 * (j % 2):256 * (j % 2) + 256], op0=ALU.mult, op1=ALU.add)
+
+        def pe_cT(t):
+            if not ok(t):
+                return
             tpb = ps_t.tile([P, 8, P], BF16, name="tpb", tag="tp")
+            cb = T[("cb", t)]
             for ch in range(8):
                 j = ch // 2
                 nc.tensor.transpose(tpb[:, ch, :], cb[:, P * ch:P * ch + P], idb[:, 32 * j:32 * j + P])
-            cg = cp.tile([P, C], BF16, name="cg", tag="cg", align_bytes=64)
-            nc.scalar.copy(out=cg[:].rearrange("p (g r t) -> p g r t", g=2, t=4), in_=tpb[:].rearrange("p (g t) r -> p g r t", g=2))
-            cq = cp.tile([P, 256], U32, name="cq", tag="cq", align_bytes=64)
-            cs = cp.tile([P, 256], U8, name="cs", tag="cs", align_bytes=64)
-            nc.vector.quantize_mx(out=cq[:].bitcast(FP8X4), scales=cs[:], in_=cg[:])
-            xt = lp.tile([P, C], BF16, name="xt", tag="xt")
-            nc.sync.dma_start(out=xt[:], in_=x[P * ib:P * ib + P, b, :])
-            xb = lp.tile([P, C], F32, name="xb", tag="xb")
-            nc.gpsimd.tensor_tensor(out=xb[:], in0=xt[:], in1=b2_bc[:], op=ALU.add)
-            v = lp.tile([P, C], F32, name="v", tag="v")
-            s2 = lp.tile([P, 2], F32, name="s2", tag="s2")
+            T[("cT", t)] = tpb
+
+        def act_cg(t):
+            if not ok(t):
+                return
+            cg = p2.tile([P, C], BF16, name="cg", tag="cg", align_bytes=64)
+            nc.scalar.copy(out=cg[:].rearrange("p (g r t) -> p g r t", g=2, t=4), in_=T[("cT", t)][:].rearrange("p (g t) r -> p g r t", g=2))
+            T[("cg", t)] = cg
+
+        def dve_qc(t):
+            if not ok(t):
+                return
+            cq = p2.tile([P, 256], U32, name="cq", tag="cq", align_bytes=64)
+            cs = p2.tile([P, 256], U8, name="cs", tag="cs", align_bytes=64)
+            nc.vector.quantize_mx(out=cq[:].bitcast(FP8X4), scales=cs[:], in_=T[("cg", t)][:])
+            T[("cq", t)] = (cq, cs)
+
+        def pe_mm2(t):
+            if not ok(t):
+                return
+            cq, cs = T[("cq", t)]
             for e2 in range(2):
                 yp = ps_y.tile([P, 512], F32, name="yp", tag="yp")
                 for g in range(2):
                     nc.tensor.matmul_mx(out=yp[:], lhsT=cq[:, P * g:P * g + P].bitcast(FP8X4), lhsT_scale=cs[:, P * g:P * g + P],
                                         rhs=w2q[:, g, 512 * e2:512 * e2 + 512].bitcast(FP8X4), rhs_scale=w2s[:, g, 512 * e2:512 * e2 + 512],
                                         start=(g == 0), stop=(g == 1))
-                nc.vector.scalar_tensor_tensor(out=v[:, 512 * e2:512 * e2 + 512], in0=yp[:], scalar=1.0, in1=xb[:, 512 * e2:512 * e2 + 512],
-                                               op0=ALU.mult, op1=ALU.add, accum_out=s2[:, e2:e2 + 1])
-            nm = lp.tile([P, 1], F32, name="nm", tag="nm")
+                T[("yp", t, e2)] = yp
+
+        def pool_xb(t):
+            if not ok(t):
+                return
+            xb = p3.tile([P, C], F32, name="xb", tag="xb")
+            nc.gpsimd.tensor_tensor(out=xb[:], in0=T[("xt", t)][:], in1=b2_bc[:], op=ALU.add)
+            T[("xb", t)] = xb
+
+        def dve_v(t):
+            if not ok(t):
+                return
+            v = p2.tile([P, C], F32, name="v", tag="v")
+            s2 = p2.tile([P, 2], F32, name="s2", tag="s2")
+            xb = T[("xb", t)]
+            for e2 in range(2):
+                nc.vector.scalar_tensor_tensor(out=v[:, 512 * e2:512 * e2 + 512], in0=T[("yp", t, e2)][:], scalar=1.0,
+                                               in1=xb[:, 512 * e2:512 * e2 + 512], op0=ALU.mult, op1=ALU.add, accum_out=s2[:, e2:e2 + 1])
+            nm = p2.tile([P, 1], F32, name="nm", tag="nm")
             nc.vector.tensor_scalar(out=nm[:], in0=s2[:, 0:1], scalar1=s2[:, 1:2], scalar2=-1.0 / C, op0=ALU.add, op1=ALU.mult)
-            junk = lp.tile([P, C], BF16, name="junk", tag="junk")
-            ss = lp.tile([P, 1], F32, name="ss", tag="ss")
-            nc.scalar.activation(out=junk[:], in_=v[:], func=ACT.Square, bias=nm[:], scale=1.0, accum_out=ss[:])
-            ve = lp.tile([P, 1], F32, name="ve", tag="ve")
-            nc.gpsimd.tensor_scalar(out=ve[:], in0=ss[:], scalar1=1.0 / C, scalar2=EPS, op0=ALU.mult, op1=ALU.add)
-            rstd = lp.tile([P, 1], F32, name="rstd", tag="rstd")
+            T[("v", t)] = v
+            T[("nm", t)] = nm
+
+        def act_sq(t):
+            if not ok(t):
+                return
+            junk = p1.tile([P, C], BF16, name="junk", tag="junk")
+            ss = p2.tile([P, 1], F32, name="ss", tag="ss")
+            nc.scalar.activation(out=junk[:], in_=T[("v", t)][:], func=ACT.Square, bias=T[("nm", t)][:], scale=1.0, accum_out=ss[:])
+            T[("ss", t)] = ss
+
+        def pool_rstd(t):
+            if not ok(t):
+                return
+            ve = p2.tile([P, 1], F32, name="ve", tag="ve")
+            nc.gpsimd.tensor_scalar(out=ve[:], in0=T[("ss", t)][:], scalar1=1.0 / C, scalar2=EPS, op0=ALU.mult, op1=ALU.add)
+            rstd = p2.tile([P, 1], F32, name="rstd", tag="rstd")
             nc.gpsimd.tensor_tensor(out=rstd[:], in0=ve[:], in1=nhalf[:], op=ALU.pow)
-            t1 = lp.tile([P, C], F32, name="t1", tag="t1")
-            nc.vector.scalar_tensor_tensor(out=t1[:], in0=v[:], scalar=nm[:], in1=g_bc[:], op0=ALU.add, op1=ALU.mult)
-            nc.vector.scalar_tensor_tensor(out=t1[:], in0=t1[:], scalar=rstd[:], in1=be_bc[:], op0=ALU.mult, op1=ALU.add)
-            nc.sync.dma_start(out=out[P * ib:P * ib + P, b, :], in_=t1[:])
+            T[("rstd", t)] = rstd
 
-        for b in range(NB):
-            phase1(0, b)
-            read_bands(0, b)
+        def dve_A(t):
+            if not ok(t):
+                return
+            t1 = p2.tile([P, C], F32, name="t1", tag="t1")
+            nc.vector.scalar_tensor_tensor(out=t1[:], in0=T[("v", t)][:], scalar=T[("nm", t)][:], in1=g_bc[:], op0=ALU.add, op1=ALU.mult)
+            T[("t1", t)] = t1
 
-        b2_bc = const.tile([P, C], BF16, name="b2_bc")
-        nc.sync.dma_start(out=b2_bc[:], in_=b2.partition_broadcast(P))
-        g_bc = const.tile([P, C], BF16, name="g_bc")
-        nc.sync.dma_start(out=g_bc[:], in_=gamma.partition_broadcast(P))
-        be_bc = const.tile([P, C], BF16, name="be_bc")
-        nc.sync.dma_start(out=be_bc[:], in_=beta.partition_broadcast(P))
-        gw2 = const.tile([P, 8192], BF16, name="gw2", align_bytes=64)
-        gw2v = gw2[:].rearrange("p (g c t) -> p g c t", g=2, t=4)
-        for rt in range(8):
+        def dve_B(t):
+            if not ok(t):
+                return
+            t1 = T[("t1", t)]
+            nc.vector.scalar_tensor_tensor(out=t1[:], in0=t1[:], scalar=T[("rstd", t)][:], in1=be_bc[:], op0=ALU.mult, op1=ALU.add)
+
+        def sp_store(t):
+            if not ok(t):
+                return
+            nc.sync.dma_start(out=out[P * (t // NB):P * (t // NB) + P, t % NB, :], in_=T[("t1", t)][:])
+
+        def w2_load(rt):
             raw = wst.tile([P, C], BF16, name="raw", tag="raw")
             nc.sync.dma_start(out=raw[:], in_=w2[P * rt:P * rt + P, :])
+            T[("raw", rt)] = raw
+
+        def w2_prep(rt):
             tpb = ps_t.tile([P, 8, P], BF16, name="tpb", tag="tp")
+            raw = T[("raw", rt)]
             for gt in range(8):
                 nc.tensor.transpose(tpb[:, gt, :], raw[:, P * gt:P * gt + P], idb[:, 0:P])
             nc.vector.tensor_copy(out=gw2v[:, :, P * rt:P * rt + P, :], in_=tpb[:].rearrange("p (g t) r -> p g r t", g=2))
-        for g in range(2):
-            nc.vector.quantize_mx(out=w2q[:, g, :].bitcast(FP8X4), scales=w2s[:, g, :], in_=gw2[:, 4096 * g:4096 * g + 4096])
 
-        for ib in range(NI):
-            for b in range(NB):
-                if ib + 1 < NI:
-                    phase1(ib + 1, b)
-                phase2a(ib, b)
-                if ib + 1 < NI:
-                    read_bands(ib + 1, b)
-                phase2b(ib, b)
+        for s in range(NT + 8):
+            ld(s + 1)
+            if s < 4:
+                w2_load(2 * s)
+                w2_load(2 * s + 1)
+            if s == 1:
+                nc.sync.dma_start(out=b2_bc[:], in_=b2.partition_broadcast(P))
+            if s == 2:
+                nc.sync.dma_start(out=g_bc[:], in_=gamma.partition_broadcast(P))
+                nc.sync.dma_start(out=be_bc[:], in_=beta.partition_broadcast(P))
+            ld_x(s - 3)
+            if (s - 3) % NB == 0 and NB <= s - 3 < NT:
+                ld_hc((s - 3) // NB)
+            sp_reads(s - 3)
+
+            pe_cT(s - 6)
+            dve_v(s - 7)
+            pe_hT(s)
+            act_cg(s - 6)
+            act_hg(s)
+            pool_hf(s)
+            pool_hcf(s - 4)
+            dve_sm1(s - 2)
+            pe_cornerT(s - 4)
+            act_lc(s - 4)
+            pe_cornermm(s - 5)
+            act_ysb(s - 5)
+            act_sq(s - 7)
+            pe_bandT(s - 4, 0)
+            act_lt(s - 4, 0)
+            pe_mm(s - 5, 0)
+            dve_A(s - 7)
+            act_exp(s - 2)
+            pe_bandT(s - 4, 1)
+            act_lt(s - 4, 1)
+            pe_mm(s - 5, 1)
+            dve_qc(s - 6)
+            dve_qh(s)
+            pool_rstd(s - 7)
+            dve_sm2(s - 2)
+            sp_write(s - 2)
+            pe_bandT(s - 4, 2)
+            act_lt(s - 4, 2)
+            pe_mm(s - 5, 2)
+            dve_c(s - 5, 0)
+            pe_bandT(s - 4, 3)
+            act_lt(s - 4, 3)
+            pe_mm(s - 5, 3)
+            dve_B(s - 7)
+            sp_store(s - 7)
+            if s < 4:
+                w2_prep(2 * s)
+                w2_prep(2 * s + 1)
+            if s == 4:
+                for g in range(2):
+                    nc.vector.quantize_mx(out=w2q[:, g, :].bitcast(FP8X4), scales=w2s[:, g, :], in_=gw2[:, 4096 * g:4096 * g + 4096])
+            pe_mm1(s - 1)
+            pe_mm2(s - 6)
+            dve_c(s - 5, 1)
+            pool_xb(s - 5)

@@ -36,9 +36,8 @@ def tile_dynamicconvdecoderlayer_pa_kernel(tc, h, x, ww, bw, w2, b2, gamma, beta
         p3 = ctx.enter_context(tc.tile_pool(name="p3", bufs=3))
         hfp = ctx.enter_context(tc.tile_pool(name="hfp", bufs=7))
         p1 = ctx.enter_context(tc.tile_pool(name="p1", bufs=1))
-        ps_t = ctx.enter_context(tc.psum_pool(name="ps_t", bufs=3))
+        ps_t = ctx.enter_context(tc.psum_pool(name="ps_t", bufs=5))
         ps_z = ctx.enter_context(tc.psum_pool(name="ps_z", bufs=1))
-        ps_c = ctx.enter_context(tc.psum_pool(name="ps_c", bufs=2))
         ps_y = ctx.enter_context(tc.psum_pool(name="ps_y", bufs=2))
         if PINNED:
             ctx.enter_context(tc.manual_schedule())
@@ -134,11 +133,11 @@ def tile_dynamicconvdecoderlayer_pa_kernel(tc, h, x, ww, bw, w2, b2, gamma, beta
                            in_=T[("hT", t)][:].rearrange("p (g u) r -> p g r u", g=2))
             T[("hg", t)] = hg
 
-        def pool_hf(t):
+        def act_hf(t):
             if not ok(t):
                 return
             hf = hfp.tile([P, C], F32, name="hf", tag="hf")
-            nc.gpsimd.tensor_scalar(out=hf[:], in0=T[("hb", t)][:], scalar1=1.0, scalar2=0.0, op0=ALU.mult, op1=ALU.add)
+            nc.scalar.copy(out=hf[:], in_=T[("hb", t)][:])
             T[("hf", t)] = hf
 
         def dve_qh(t):
@@ -166,8 +165,14 @@ def tile_dynamicconvdecoderlayer_pa_kernel(tc, h, x, ww, bw, w2, b2, gamma, beta
             nc.vector.tensor_tensor(out=zb[:].rearrange("p n k -> p (n k)"), in0=T[("z", t)][:], in1=bw_bc[:], op=ALU.add)
             mx = p2.tile([P, H], F32, name="mx", tag="mx")
             nc.vector.tensor_reduce(out=mx[:], in_=zb[:], axis=AX.X, op=ALU.max)
-            nc.vector.tensor_tensor(out=zb[:], in0=zb[:], in1=mx[:].unsqueeze(2).to_broadcast([P, H, K]), op=ALU.subtract)
             T[("zb", t)] = zb
+            T[("mx", t)] = mx
+
+        def pool_sub(t):
+            if not ok(t):
+                return
+            zb = T[("zb", t)]
+            nc.gpsimd.tensor_tensor(out=zb[:], in0=zb[:], in1=T[("mx", t)][:].unsqueeze(2).to_broadcast([P, H, K]), op=ALU.subtract)
 
         def act_exp(t):
             if not ok(t):
@@ -184,8 +189,15 @@ def tile_dynamicconvdecoderlayer_pa_kernel(tc, h, x, ww, bw, w2, b2, gamma, beta
             nc.vector.tensor_reduce(out=sums[:], in_=ex[:], axis=AX.X, op=ALU.add)
             rs = p2.tile([P, H], F32, name="rs", tag="rs")
             nc.vector.reciprocal(out=rs[:], in_=sums[:])
+            T[("rs", t)] = rs
+
+        def pool_mult(t):
+            if not ok(t):
+                return
+            ex = T[("ex", t)]
+            rs = T[("rs", t)]
             sv = stages[t % 3][:, 0:H * CH].rearrange("p (n c) -> p n c", c=CH)
-            nc.vector.tensor_tensor(out=sv[:, :, 0:K], in0=ex[:], in1=rs[:].unsqueeze(2).to_broadcast([P, H, K]), op=ALU.mult)
+            nc.gpsimd.tensor_tensor(out=sv[:, :, 0:K], in0=ex[:], in1=rs[:].unsqueeze(2).to_broadcast([P, H, K]), op=ALU.mult)
 
         def sp_write(t):
             if not ok(t):
@@ -223,11 +235,11 @@ def tile_dynamicconvdecoderlayer_pa_kernel(tc, h, x, ww, bw, w2, b2, gamma, beta
             nc.scalar.copy(out=lc[:], in_=T[("lcT", t)][:])
             T[("lc", t)] = lc
 
-        def pool_hcf(t):
+        def act_hcf(t):
             if not ok(t) or t < NB:
                 return
             hcf = p2.tile([P, 256], F32, name="hcf", tag="hcf")
-            nc.gpsimd.tensor_scalar(out=hcf[:], in0=T[("hcb", t // NB)][:, t % NB, :], scalar1=1.0, scalar2=0.0, op0=ALU.mult, op1=ALU.add)
+            nc.scalar.copy(out=hcf[:], in_=T[("hcb", t // NB)][:, t % NB, :])
             T[("hcf", t)] = hcf
 
         def pe_cornermm(t):
@@ -267,7 +279,7 @@ def tile_dynamicconvdecoderlayer_pa_kernel(tc, h, x, ww, bw, w2, b2, gamma, beta
             if not ok(t):
                 return
             if j % 2 == 0:
-                T[("cd", t, j // 2)] = ps_c.tile([P, 512], F32, name="cd", tag="cd")
+                T[("cd", t, j // 2)] = ps_t.tile([P, 512], F32, name="cd", tag="tp")
             cd = T[("cd", t, j // 2)]
             lt = T[("lt", t)]
             hf = T[("hf", t)]
@@ -411,47 +423,49 @@ def tile_dynamicconvdecoderlayer_pa_kernel(tc, h, x, ww, bw, w2, b2, gamma, beta
             sp_reads(s - 3)
 
             pe_cT(s - 6)
-            dve_v(s - 7)
             pe_hT(s)
+            pe_cornerT(s - 4)
+            dve_v(s - 7)
             act_cg(s - 6)
             act_hg(s)
-            pool_hf(s)
-            pool_hcf(s - 4)
             dve_sm1(s - 2)
-            pe_cornerT(s - 4)
-            act_lc(s - 4)
-            pe_cornermm(s - 5)
-            act_ysb(s - 5)
+            pool_sub(s - 2)
             act_sq(s - 7)
+            act_lc(s - 4)
             pe_bandT(s - 4, 0)
             act_lt(s - 4, 0)
-            pe_mm(s - 5, 0)
             dve_A(s - 7)
             act_exp(s - 2)
             pe_bandT(s - 4, 1)
             act_lt(s - 4, 1)
-            pe_mm(s - 5, 1)
             dve_qc(s - 6)
             dve_qh(s)
             pool_rstd(s - 7)
-            dve_sm2(s - 2)
-            sp_write(s - 2)
             pe_bandT(s - 4, 2)
             act_lt(s - 4, 2)
-            pe_mm(s - 5, 2)
-            dve_c(s - 5, 0)
+            dve_sm2(s - 2)
+            pool_mult(s - 2)
+            sp_write(s - 2)
             pe_bandT(s - 4, 3)
             act_lt(s - 4, 3)
-            pe_mm(s - 5, 3)
+            pe_cornermm(s - 5)
+            act_ysb(s - 5)
+            pe_mm(s - 5, 0)
+            pe_mm(s - 5, 1)
             dve_B(s - 7)
             sp_store(s - 7)
+            dve_c(s - 5, 0)
+            pe_mm(s - 5, 2)
+            pe_mm(s - 5, 3)
+            act_hf(s)
+            act_hcf(s - 4)
+            pe_mm1(s - 1)
             if s < 4:
                 w2_prep(2 * s)
                 w2_prep(2 * s + 1)
             if s == 4:
                 for g in range(2):
                     nc.vector.quantize_mx(out=w2q[:, g, :].bitcast(FP8X4), scales=w2s[:, g, :], in_=gw2[:, 4096 * g:4096 * g + 4096])
-            pe_mm1(s - 1)
             pe_mm2(s - 6)
             dve_c(s - 5, 1)
             pool_xb(s - 5)

@@ -133,11 +133,11 @@ def tile_dynamicconvdecoderlayer_pa_kernel(tc, h, x, ww, bw, w2, b2, gamma, beta
                            in_=T[("hT", t)][:].rearrange("p (g u) r -> p g r u", g=2))
             T[("hg", t)] = hg
 
-        def act_hf(t):
+        def pool_hf(t):
             if not ok(t):
                 return
             hf = hfp.tile([P, C], F32, name="hf", tag="hf")
-            nc.scalar.copy(out=hf[:], in_=T[("hb", t)][:])
+            nc.gpsimd.tensor_scalar(out=hf[:], in0=T[("hb", t)][:], scalar1=1.0, scalar2=0.0, op0=ALU.mult, op1=ALU.add)
             T[("hf", t)] = hf
 
         def dve_qh(t):
@@ -165,14 +165,8 @@ def tile_dynamicconvdecoderlayer_pa_kernel(tc, h, x, ww, bw, w2, b2, gamma, beta
             nc.vector.tensor_tensor(out=zb[:].rearrange("p n k -> p (n k)"), in0=T[("z", t)][:], in1=bw_bc[:], op=ALU.add)
             mx = p2.tile([P, H], F32, name="mx", tag="mx")
             nc.vector.tensor_reduce(out=mx[:], in_=zb[:], axis=AX.X, op=ALU.max)
+            nc.vector.tensor_tensor(out=zb[:], in0=zb[:], in1=mx[:].unsqueeze(2).to_broadcast([P, H, K]), op=ALU.subtract)
             T[("zb", t)] = zb
-            T[("mx", t)] = mx
-
-        def pool_sub(t):
-            if not ok(t):
-                return
-            zb = T[("zb", t)]
-            nc.gpsimd.tensor_tensor(out=zb[:], in0=zb[:], in1=T[("mx", t)][:].unsqueeze(2).to_broadcast([P, H, K]), op=ALU.subtract)
 
         def act_exp(t):
             if not ok(t):
@@ -189,15 +183,8 @@ def tile_dynamicconvdecoderlayer_pa_kernel(tc, h, x, ww, bw, w2, b2, gamma, beta
             nc.vector.tensor_reduce(out=sums[:], in_=ex[:], axis=AX.X, op=ALU.add)
             rs = p2.tile([P, H], F32, name="rs", tag="rs")
             nc.vector.reciprocal(out=rs[:], in_=sums[:])
-            T[("rs", t)] = rs
-
-        def pool_mult(t):
-            if not ok(t):
-                return
-            ex = T[("ex", t)]
-            rs = T[("rs", t)]
             sv = stages[t % 3][:, 0:H * CH].rearrange("p (n c) -> p n c", c=CH)
-            nc.gpsimd.tensor_tensor(out=sv[:, :, 0:K], in0=ex[:], in1=rs[:].unsqueeze(2).to_broadcast([P, H, K]), op=ALU.mult)
+            nc.vector.tensor_tensor(out=sv[:, :, 0:K], in0=ex[:], in1=rs[:].unsqueeze(2).to_broadcast([P, H, K]), op=ALU.mult)
 
         def sp_write(t):
             if not ok(t):
@@ -235,11 +222,11 @@ def tile_dynamicconvdecoderlayer_pa_kernel(tc, h, x, ww, bw, w2, b2, gamma, beta
             nc.scalar.copy(out=lc[:], in_=T[("lcT", t)][:])
             T[("lc", t)] = lc
 
-        def act_hcf(t):
+        def pool_hcf(t):
             if not ok(t) or t < NB:
                 return
             hcf = p2.tile([P, 256], F32, name="hcf", tag="hcf")
-            nc.scalar.copy(out=hcf[:], in_=T[("hcb", t // NB)][:, t % NB, :])
+            nc.gpsimd.tensor_scalar(out=hcf[:], in0=T[("hcb", t // NB)][:, t % NB, :], scalar1=1.0, scalar2=0.0, op0=ALU.mult, op1=ALU.add)
             T[("hcf", t)] = hcf
 
         def pe_cornermm(t):
@@ -425,40 +412,34 @@ def tile_dynamicconvdecoderlayer_pa_kernel(tc, h, x, ww, bw, w2, b2, gamma, beta
             pe_cT(s - 6)
             pe_hT(s)
             pe_cornerT(s - 4)
+            for j in range(4):
+                pe_bandT(s - 4, j)
             dve_v(s - 7)
             act_cg(s - 6)
             act_hg(s)
-            dve_sm1(s - 2)
-            pool_sub(s - 2)
-            act_sq(s - 7)
             act_lc(s - 4)
-            pe_bandT(s - 4, 0)
-            act_lt(s - 4, 0)
+            for j in range(4):
+                act_lt(s - 4, j)
+            pool_hf(s)
+            pool_hcf(s - 4)
+            dve_sm1(s - 2)
             dve_A(s - 7)
-            act_exp(s - 2)
-            pe_bandT(s - 4, 1)
-            act_lt(s - 4, 1)
             dve_qc(s - 6)
             dve_qh(s)
-            pool_rstd(s - 7)
-            pe_bandT(s - 4, 2)
-            act_lt(s - 4, 2)
-            dve_sm2(s - 2)
-            pool_mult(s - 2)
-            sp_write(s - 2)
-            pe_bandT(s - 4, 3)
-            act_lt(s - 4, 3)
             pe_cornermm(s - 5)
             act_ysb(s - 5)
+            act_exp(s - 2)
+            act_sq(s - 7)
+            pool_rstd(s - 7)
             pe_mm(s - 5, 0)
             pe_mm(s - 5, 1)
-            dve_B(s - 7)
-            sp_store(s - 7)
+            dve_sm2(s - 2)
+            sp_write(s - 2)
             dve_c(s - 5, 0)
             pe_mm(s - 5, 2)
             pe_mm(s - 5, 3)
-            act_hf(s)
-            act_hcf(s - 4)
+            dve_B(s - 7)
+            sp_store(s - 7)
             pe_mm1(s - 1)
             if s < 4:
                 w2_prep(2 * s)

@@ -36,8 +36,9 @@ def tile_dynamicconvdecoderlayer_pa_kernel(tc, h, x, ww, bw, w2, b2, gamma, beta
         p3 = ctx.enter_context(tc.tile_pool(name="p3", bufs=3))
         hfp = ctx.enter_context(tc.tile_pool(name="hfp", bufs=7))
         p1 = ctx.enter_context(tc.tile_pool(name="p1", bufs=1))
-        ps_t = ctx.enter_context(tc.psum_pool(name="ps_t", bufs=5))
+        ps_t = ctx.enter_context(tc.psum_pool(name="ps_t", bufs=3))
         ps_z = ctx.enter_context(tc.psum_pool(name="ps_z", bufs=1))
+        ps_c = ctx.enter_context(tc.psum_pool(name="ps_c", bufs=2))
         ps_y = ctx.enter_context(tc.psum_pool(name="ps_y", bufs=2))
         if PINNED:
             ctx.enter_context(tc.manual_schedule())
@@ -112,9 +113,6 @@ def tile_dynamicconvdecoderlayer_pa_kernel(tc, h, x, ww, bw, w2, b2, gamma, beta
                 nc.scalar.copy(out=gww32[:, :, P * rt:P * rt + P, :], in_=tp[:].rearrange("p (g u) r -> p g r u", g=2))
         for g in range(2):
             nc.vector.quantize_mx(out=wwq[:, g, :].bitcast(FP8X4), scales=wws[:, g, :], in_=gww[:, 2048 * g:2048 * g + 2048])
-        for i in range(NBAND):
-            nc.vector.memset(bands[i][:], 0.0)
-            nc.vector.memset(corners[i][:], 0.0)
 
         def pe_hT(t):
             if not ok(t):
@@ -137,7 +135,7 @@ def tile_dynamicconvdecoderlayer_pa_kernel(tc, h, x, ww, bw, w2, b2, gamma, beta
             if not ok(t):
                 return
             hf = hfp.tile([P, C], F32, name="hf", tag="hf")
-            nc.gpsimd.tensor_scalar(out=hf[:], in0=T[("hb", t)][:], scalar1=1.0, scalar2=0.0, op0=ALU.mult, op1=ALU.add)
+            nc.scalar.copy(out=hf[:], in_=T[("hb", t)][:])
             T[("hf", t)] = hf
 
         def dve_qh(t):
@@ -226,7 +224,7 @@ def tile_dynamicconvdecoderlayer_pa_kernel(tc, h, x, ww, bw, w2, b2, gamma, beta
             if not ok(t) or t < NB:
                 return
             hcf = p2.tile([P, 256], F32, name="hcf", tag="hcf")
-            nc.gpsimd.tensor_scalar(out=hcf[:], in0=T[("hcb", t // NB)][:, t % NB, :], scalar1=1.0, scalar2=0.0, op0=ALU.mult, op1=ALU.add)
+            nc.scalar.copy(out=hcf[:], in_=T[("hcb", t // NB)][:, t % NB, :])
             T[("hcf", t)] = hcf
 
         def pe_cornermm(t):
@@ -266,7 +264,7 @@ def tile_dynamicconvdecoderlayer_pa_kernel(tc, h, x, ww, bw, w2, b2, gamma, beta
             if not ok(t):
                 return
             if j % 2 == 0:
-                T[("cd", t, j // 2)] = ps_t.tile([P, 512], F32, name="cd", tag="tp")
+                T[("cd", t, j // 2)] = ps_c.tile([P, 512], F32, name="cd", tag="cd")
             cd = T[("cd", t, j // 2)]
             lt = T[("lt", t)]
             hf = T[("hf", t)]
@@ -330,7 +328,7 @@ def tile_dynamicconvdecoderlayer_pa_kernel(tc, h, x, ww, bw, w2, b2, gamma, beta
             if not ok(t):
                 return
             xb = p3.tile([P, C], F32, name="xb", tag="xb")
-            nc.gpsimd.tensor_tensor(out=xb[:], in0=T[("xt", t)][:], in1=b2_bc[:], op=ALU.add)
+            nc.vector.tensor_tensor(out=xb[:], in0=T[("xt", t)][:], in1=b2_bc[:], op=ALU.add)
             T[("xb", t)] = xb
 
         def dve_v(t):
@@ -392,7 +390,7 @@ def tile_dynamicconvdecoderlayer_pa_kernel(tc, h, x, ww, bw, w2, b2, gamma, beta
             raw = T[("raw", rt)]
             for gt in range(8):
                 nc.tensor.transpose(tpb[:, gt, :], raw[:, P * gt:P * gt + P], idb[:, 0:P])
-            nc.vector.tensor_copy(out=gw2v[:, :, P * rt:P * rt + P, :], in_=tpb[:].rearrange("p (g t) r -> p g r t", g=2))
+            nc.scalar.copy(out=gw2v[:, :, P * rt:P * rt + P, :], in_=tpb[:].rearrange("p (g t) r -> p g r t", g=2))
 
         for s in range(NT + 8):
             ld(s + 1)
@@ -410,40 +408,48 @@ def tile_dynamicconvdecoderlayer_pa_kernel(tc, h, x, ww, bw, w2, b2, gamma, beta
             sp_reads(s - 3)
 
             pe_cT(s - 6)
-            pe_hT(s)
-            pe_cornerT(s - 4)
-            for j in range(4):
-                pe_bandT(s - 4, j)
             dve_v(s - 7)
+            pe_hT(s)
             act_cg(s - 6)
             act_hg(s)
-            act_lc(s - 4)
-            for j in range(4):
-                act_lt(s - 4, j)
-            pool_hf(s)
-            pool_hcf(s - 4)
             dve_sm1(s - 2)
-            dve_A(s - 7)
-            dve_qc(s - 6)
-            dve_qh(s)
+            pe_cornerT(s - 4)
+            act_lc(s - 4)
             pe_cornermm(s - 5)
             act_ysb(s - 5)
-            act_exp(s - 2)
-            act_sq(s - 7)
-            pool_rstd(s - 7)
+
+            pe_bandT(s - 4, 0)
+            act_lt(s - 4, 0)
             pe_mm(s - 5, 0)
+            dve_A(s - 7)
+            act_sq(s - 7)
+            pe_bandT(s - 4, 1)
+            act_lt(s - 4, 1)
             pe_mm(s - 5, 1)
+            act_exp(s - 2)
+            dve_qc(s - 6)
+            dve_qh(s)
+            pool_rstd(s - 7)
             dve_sm2(s - 2)
             sp_write(s - 2)
-            dve_c(s - 5, 0)
+            pe_bandT(s - 4, 2)
+            act_lt(s - 4, 2)
             pe_mm(s - 5, 2)
+            dve_c(s - 5, 0)
+            pe_bandT(s - 4, 3)
+            act_lt(s - 4, 3)
             pe_mm(s - 5, 3)
             dve_B(s - 7)
             sp_store(s - 7)
+            pool_hf(s)
+            pool_hcf(s - 4)
             pe_mm1(s - 1)
             if s < 4:
                 w2_prep(2 * s)
                 w2_prep(2 * s + 1)
+            if s < NBAND:
+                nc.vector.memset(bands[s][:], 0.0)
+                nc.vector.memset(corners[s][:], 0.0)
             if s == 4:
                 for g in range(2):
                     nc.vector.quantize_mx(out=w2q[:, g, :].bitcast(FP8X4), scales=w2s[:, g, :], in_=gw2[:, 4096 * g:4096 * g + 4096])

@@ -31,7 +31,7 @@ def tile_dynamicconvdecoderlayer_pa_kernel(tc, h, x, ww, bw, w2, b2, gamma, beta
     nc = tc.nc
     with ExitStack() as ctx:
         const = ctx.enter_context(tc.tile_pool(name="const", bufs=1))
-        wst = ctx.enter_context(tc.tile_pool(name="wst", bufs=2))
+        wst = ctx.enter_context(tc.tile_pool(name="wst", bufs=4))
         p2 = ctx.enter_context(tc.tile_pool(name="p2", bufs=2))
         p3 = ctx.enter_context(tc.tile_pool(name="p3", bufs=3))
         hfp = ctx.enter_context(tc.tile_pool(name="hfp", bufs=7))
@@ -96,7 +96,7 @@ def tile_dynamicconvdecoderlayer_pa_kernel(tc, h, x, ww, bw, w2, b2, gamma, beta
 
         raws = []
         for rt in range(4):
-            raw = p1.tile([P, C], BF16, name="rawww%d" % rt)
+            raw = wst.tile([P, C], BF16, name="raw", tag="raw")
             nc.sync.dma_start(out=raw[:], in_=ww[P * rt:P * rt + P, :])
             raws.append(raw)
         ld(0)
@@ -113,6 +113,7 @@ def tile_dynamicconvdecoderlayer_pa_kernel(tc, h, x, ww, bw, w2, b2, gamma, beta
                 nc.scalar.copy(out=gww32[:, :, P * rt:P * rt + P, :], in_=tp[:].rearrange("p (g u) r -> p g r u", g=2))
         for g in range(2):
             nc.vector.quantize_mx(out=wwq[:, g, :].bitcast(FP8X4), scales=wws[:, g, :], in_=gww[:, 2048 * g:2048 * g + 2048])
+        nc.vector.memset(bands[0][:], 0.0)
 
         def pe_hT(t):
             if not ok(t):
@@ -394,9 +395,9 @@ def tile_dynamicconvdecoderlayer_pa_kernel(tc, h, x, ww, bw, w2, b2, gamma, beta
 
         for s in range(NT + 8):
             ld(s + 1)
-            if s < 4:
-                w2_load(2 * s)
-                w2_load(2 * s + 1)
+            if 1 - 1 <= s < 1 + 3:
+                w2_load(2 * (s - 1 + 1))
+                w2_load(2 * (s - 1 + 1) + 1)
             if s == 1:
                 nc.sync.dma_start(out=b2_bc[:], in_=b2.partition_broadcast(P))
             if s == 2:
@@ -407,35 +408,35 @@ def tile_dynamicconvdecoderlayer_pa_kernel(tc, h, x, ww, bw, w2, b2, gamma, beta
                 ld_hc((s - 3) // NB)
             sp_reads(s - 3)
 
+            pe_mm(s - 5, 0)
             pe_cT(s - 6)
             dve_v(s - 7)
-            pe_hT(s)
             act_cg(s - 6)
+            pe_mm(s - 5, 1)
+            pe_hT(s)
             act_hg(s)
-            dve_sm1(s - 2)
             pe_cornerT(s - 4)
             act_lc(s - 4)
+            dve_sm1(s - 2)
+            dve_qc(s - 6)
             pe_cornermm(s - 5)
             act_ysb(s - 5)
-
+            act_sq(s - 7)
             pe_bandT(s - 4, 0)
             act_lt(s - 4, 0)
-            pe_mm(s - 5, 0)
             dve_A(s - 7)
-            act_sq(s - 7)
+            pool_xb(s - 5)
             pe_bandT(s - 4, 1)
             act_lt(s - 4, 1)
-            pe_mm(s - 5, 1)
             act_exp(s - 2)
-            dve_qc(s - 6)
+            dve_c(s - 5, 0)
             dve_qh(s)
             pool_rstd(s - 7)
+            pe_mm(s - 5, 2)
             dve_sm2(s - 2)
             sp_write(s - 2)
             pe_bandT(s - 4, 2)
             act_lt(s - 4, 2)
-            pe_mm(s - 5, 2)
-            dve_c(s - 5, 0)
             pe_bandT(s - 4, 3)
             act_lt(s - 4, 3)
             pe_mm(s - 5, 3)
@@ -444,15 +445,16 @@ def tile_dynamicconvdecoderlayer_pa_kernel(tc, h, x, ww, bw, w2, b2, gamma, beta
             pool_hf(s)
             pool_hcf(s - 4)
             pe_mm1(s - 1)
-            if s < 4:
-                w2_prep(2 * s)
-                w2_prep(2 * s + 1)
-            if s < NBAND:
-                nc.vector.memset(bands[s][:], 0.0)
-                nc.vector.memset(corners[s][:], 0.0)
-            if s == 4:
-                for g in range(2):
-                    nc.vector.quantize_mx(out=w2q[:, g, :].bitcast(FP8X4), scales=w2s[:, g, :], in_=gw2[:, 4096 * g:4096 * g + 4096])
             pe_mm2(s - 6)
             dve_c(s - 5, 1)
-            pool_xb(s - 5)
+            if 1 <= s < 1 + 4:
+                w2_prep(2 * (s - 1))
+                w2_prep(2 * (s - 1) + 1)
+            if 2 <= s < 4:
+                nc.vector.memset(bands[s - 1][:], 0.0)
+            if s == 4:
+                for ct in corners:
+                    nc.vector.memset(ct[:], 0.0)
+            if s == 1 + 4:
+                for g in range(2):
+                    nc.vector.quantize_mx(out=w2q[:, g, :].bitcast(FP8X4), scales=w2s[:, g, :], in_=gw2[:, 4096 * g:4096 * g + 4096])

@@ -24,7 +24,7 @@ R = 64
 CH = 63
 EPS = 1e-5
 NBAND = 3
-PINNED = True
+PINNED = False
 
 
 def tile_dynamicconvdecoderlayer_pa_kernel(tc, h, x, ww, bw, w2, b2, gamma, beta, out):

@@ -24,7 +24,7 @@ R = 64
 CH = 63
 EPS = 1e-5
 NBAND = 3
-PINNED = False
+PINNED = True
 
 
 def tile_dynamicconvdecoderlayer_pa_kernel(tc, h, x, ww, bw, w2, b2, gamma, beta, out):
@@ -72,7 +72,7 @@ def tile_dynamicconvdecoderlayer_pa_kernel(tc, h, x, ww, bw, w2, b2, gamma, beta
         gw2v = gw2[:].rearrange("p (g c t) -> p g c t", g=2, t=4)
         stages = [const.tile([P, 1024], F32, name="stage%d" % i) for i in range(3)]
         bands = [const.tile([P, H, P], F32, name="band%d" % i) for i in range(NBAND)]
-        corners = [const.tile([P, 4, P], F32, name="corner%d" % i) for i in range(NBAND)]
+        corners = [const.tile([P, 4, P], F32, name="corner%d" % i, align_bytes=64) for i in range(NBAND)]
 
         def ld(t):
             if not ok(t):
@@ -206,19 +206,11 @@ def tile_dynamicconvdecoderlayer_pa_kernel(tc, h, x, ww, bw, w2, b2, gamma, beta
                 else:
                     nc.sync.dma_start(out=bt[32 * a:32 * a + 32, :, 32 * (a - 1) + 1:32 * (a - 1) + 64], in_=src[:, :, 0:63])
 
-        def pe_cornerT(t):
+        def dve_lc(t):
             if not ok(t) or t < NB:
                 return
-            tp = ps_t.tile([P, 4, P], F32, name="tp", tag="tp")
-            for q in range(4):
-                nc.tensor.transpose(tp[:, q, :], corners[t % NBAND][:, q, :], idf[:, 0:P])
-            T[("lcT", t)] = tp
-
-        def act_lc(t):
-            if not ok(t) or t < NB:
-                return
-            lc = p2.tile([P, 4, P], F32, name="lc", tag="lc")
-            nc.scalar.copy(out=lc[:], in_=T[("lcT", t)][:])
+            lc = p2.tile([P, 4, P], F32, name="lc", tag="lc", align_bytes=64)
+            nc.vector.transpose(out=lc[:].rearrange("p q c -> p (q c)"), in_=corners[t % NBAND][:].rearrange("p q c -> p (q c)"))
             T[("lc", t)] = lc
 
         def pool_hcf(t):
@@ -415,8 +407,6 @@ def tile_dynamicconvdecoderlayer_pa_kernel(tc, h, x, ww, bw, w2, b2, gamma, beta
             pe_mm(s - 5, 1)
             pe_hT(s)
             act_hg(s)
-            pe_cornerT(s - 4)
-            act_lc(s - 4)
             dve_sm1(s - 2)
             dve_qc(s - 6)
             pe_cornermm(s - 5)
@@ -431,6 +421,7 @@ def tile_dynamicconvdecoderlayer_pa_kernel(tc, h, x, ww, bw, w2, b2, gamma, beta
             act_exp(s - 2)
             dve_c(s - 5, 0)
             dve_qh(s)
+            dve_lc(s - 4)
             pool_rstd(s - 7)
             pe_mm(s - 5, 2)
             dve_sm2(s - 2)

from contextlib import ExitStack

import concourse.mybir as mybir
from concourse.masks import make_identity

FLOPS = 6576668672
F32 = mybir.dt.float32
BF16 = mybir.dt.bfloat16
U32 = mybir.dt.uint32
U8 = mybir.dt.uint8
FP8X4 = mybir.dt.float8_e4m3fn_x4
ALU = mybir.AluOpType
ACT = mybir.ActivationFunctionType
AX = mybir.AxisListType

P = 128
NB = 4
NI = 4
NT = NB * NI
C = 1024
H = 16
K = 32
R = 64
CH = 63
EPS = 1e-5
NBAND = 3
PINNED = True


def tile_dynamicconvdecoderlayer_pa_kernel(tc, h, x, ww, bw, w2, b2, gamma, beta, out):
    nc = tc.nc
    with ExitStack() as ctx:
        const = ctx.enter_context(tc.tile_pool(name="const", bufs=1))
        wst = ctx.enter_context(tc.tile_pool(name="wst", bufs=4))
        p2 = ctx.enter_context(tc.tile_pool(name="p2", bufs=2))
        p3 = ctx.enter_context(tc.tile_pool(name="p3", bufs=3))
        hfp = ctx.enter_context(tc.tile_pool(name="hfp", bufs=7))
        p1 = ctx.enter_context(tc.tile_pool(name="p1", bufs=1))
        ps_t = ctx.enter_context(tc.psum_pool(name="ps_t", bufs=3))
        ps_z = ctx.enter_context(tc.psum_pool(name="ps_z", bufs=1))
        ps_c = ctx.enter_context(tc.psum_pool(name="ps_c", bufs=2))
        ps_y = ctx.enter_context(tc.psum_pool(name="ps_y", bufs=2))
        if PINNED:
            ctx.enter_context(tc.manual_schedule())

        flat = out.rearrange("t b e -> (t b e)")
        T = {}

        def ok(t):
            return 0 <= t < NT

        idf = const.tile([P, 2 * P], F32, name="idf")
        make_identity(nc, idf[:, 0:P])
        nc.vector.tensor_copy(out=idf[:, P:2 * P], in_=idf[:, 0:P])
        idb = const.tile([P, 2 * P], BF16, name="idb")
        nc.vector.tensor_copy(out=idb[:], in_=idf[:])
        msk = const.tile([P, 4], F32, name="msk")
        nc.vector.tensor_reduce(out=msk[:], in_=idf[:, 0:P].rearrange("p (j c) -> p j c", c=32), axis=AX.X, op=ALU.add)
        nhalf = const.tile([P, 1], F32, name="nhalf")
        nc.vector.memset(nhalf[:], -0.5)
        bw_bc = const.tile([P, H * K], BF16, name="bw_bc")
        b2_bc = const.tile([P, C], BF16, name="b2_bc")
        g_bc = const.tile([P, C], BF16, name="g_bc")
        be_bc = const.tile([P, C], BF16, name="be_bc")
        wwq = const.tile([P, 2, 512], U32, name="wwq", align_bytes=64)
        wws = const.tile([P, 2, 512], U8, name="wws", align_bytes=64)
        w2q = const.tile([P, 2, 1024], U32, name="w2q", align_bytes=64)
        w2s = const.tile([P, 2, 1024], U8, name="w2s", align_bytes=64)
        gww = const.tile([P, 4096], BF16, name="gww", align_bytes=64)
        gww32 = gww[:].bitcast(F32).rearrange("p (g c u) -> p g c u", g=2, u=2)
        gw2 = const.tile([P, 8192], BF16, name="gw2", align_bytes=64)
        gw2v = gw2[:].rearrange("p (g c t) -> p g c t", g=2, t=4)
        stages = [const.tile([P, 1024], F32, name="stage%d" % i) for i in range(3)]
        bands = [const.tile([P, H, P], F32, name="band%d" % i) for i in range(NBAND)]
        corners = [const.tile([P, 4, P], F32, name="corner%d" % i, align_bytes=64) for i in range(NBAND)]

        def ld(t):
            if not ok(t):
                return
            hb = p3.tile([P, C], BF16, name="hb", tag="hb")
            nc.sync.dma_start(out=hb[:], in_=h[P * (t // NB):P * (t // NB) + P, t % NB, :])
            T[("hb", t)] = hb

        def ld_x(t):
            if not ok(t):
                return
            xt = p3.tile([P, C], BF16, name="xt", tag="xt")
            nc.sync.dma_start(out=xt[:], in_=x[P * (t // NB):P * (t // NB) + P, t % NB, :])
            T[("xt", t)] = xt

        def ld_hc(ib):
            hcb = p2.tile([P, NB, 256], BF16, name="hcb", tag="hcb")
            for j in range(4):
                nc.sync.dma_start(out=hcb[32 * j:32 * j + 32, :, :], in_=h[P * ib - 32:P * ib, :, 256 * j:256 * j + 256])
            T[("hcb", ib)] = hcb

        raws = []
        for rt in range(4):
            raw = wst.tile([P, C], BF16, name="raw", tag="raw")
            nc.sync.dma_start(out=raw[:], in_=ww[P * rt:P * rt + P, :])
            raws.append(raw)
        ld(0)
        nc.sync.dma_start(out=bw_bc[:], in_=bw.partition_broadcast(P))
        for st in stages:
            nc.vector.memset(st[:], 0.0)
        for rt in range(4):
            tp = ps_t.tile([P, 4, P], F32, name="tp", tag="tp")
            for gu in range(4):
                nc.tensor.transpose(tp[:, gu, :], raws[rt][:].bitcast(F32)[:, P * gu:P * gu + P], idf[:, 0:P])
            if rt % 2 == 0:
                nc.vector.tensor_copy(out=gww32[:, :, P * rt:P * rt + P, :], in_=tp[:].rearrange("p (g u) r -> p g r u", g=2))
            else:
                nc.scalar.copy(out=gww32[:, :, P * rt:P * rt + P, :], in_=tp[:].rearrange("p (g u) r -> p g r u", g=2))
        for g in range(2):
            nc.vector.quantize_mx(out=wwq[:, g, :].bitcast(FP8X4), scales=wws[:, g, :], in_=gww[:, 2048 * g:2048 * g + 2048])
        nc.vector.memset(bands[0][:], 0.0)

        def pe_hT(t):
            if not ok(t):
                return
            tp = ps_t.tile([P, 4, P], F32, name="tp", tag="tp")
            hb = T[("hb", t)]
            for gu in range(4):
                nc.tensor.transpose(tp[:, gu, :], hb[:].bitcast(F32)[:, P * gu:P * gu + P], idf[:, 0:P])
            T[("hT", t)] = tp

        def act_hg(t):
            if not ok(t):
                return
            hg = p2.tile([P, C], BF16, name="hg", tag="hg", align_bytes=64)
            nc.scalar.copy(out=hg[:].bitcast(F32).rearrange("p (g r u) -> p g r u", g=2, u=2),
                           in_=T[("hT", t)][:].rearrange("p (g u) r -> p g r u", g=2))
            T[("hg", t)] = hg

        def pool_hf(t):
            if not ok(t):
                return
            hf = hfp.tile([P, C], F32, name="hf", tag="hf")
            nc.scalar.copy(out=hf[:], in_=T[("hb", t)][:])
            T[("hf", t)] = hf

        def dve_qh(t):
            if not ok(t):
                return
            hq = p3.tile([P, 256], U32, name="hq", tag="hq", align_bytes=64)
            hs = p3.tile([P, 256], U8, name="hs", tag="hs", align_bytes=64)
            nc.vector.quantize_mx(out=hq[:].bitcast(FP8X4), scales=hs[:], in_=T[("hg", t)][:])
            T[("hq", t)] = (hq, hs)

        def pe_mm1(t):
            if not ok(t):
                return
            hq, hs = T[("hq", t)]
            z = ps_z.tile([P, 512], F32, name="z", tag="z")
            for g in range(2):
                nc.tensor.matmul_mx(out=z[:], lhsT=hq[:, P * g:P * g + P].bitcast(FP8X4), lhsT_scale=hs[:, P * g:P * g + P],
                                    rhs=wwq[:, g, :].bitcast(FP8X4), rhs_scale=wws[:, g, :], start=(g == 0), stop=(g == 1))
            T[("z", t)] = z

        def dve_sm1(t):
            if not ok(t):
                return
            zb = p2.tile([P, H, K], F32, name="zb", tag="zb")
            nc.vector.tensor_tensor(out=zb[:].rearrange("p n k -> p (n k)"), in0=T[("z", t)][:], in1=bw_bc[:], op=ALU.add)
            mx = p2.tile([P, H], F32, name="mx", tag="mx")
            nc.vector.tensor_reduce(out=mx[:], in_=zb[:], axis=AX.X, op=ALU.max)
            nc.vector.tensor_tensor(out=zb[:], in0=zb[:], in1=mx[:].unsqueeze(2).to_broadcast([P, H, K]), op=ALU.subtract)
            T[("zb", t)] = zb

        def act_exp(t):
            if not ok(t):
                return
            ex = p2.tile([P, H, K], F32, name="ex", tag="ex")
            nc.scalar.activation(out=ex[:], in_=T[("zb", t)][:], func=ACT.Exp)
            T[("ex", t)] = ex

        def dve_sm2(t):
            if not ok(t):
                return
            ex = T[("ex", t)]
            sums = p2.tile([P, H], F32, name="sums", tag="sums")
            nc.vector.tensor_reduce(out=sums[:], in_=ex[:], axis=AX.X, op=ALU.add)
            rs = p2.tile([P, H], F32, name="rs", tag="rs")
            nc.vector.reciprocal(out=rs[:], in_=sums[:])
            sv = stages[t % 3][:, 0:H * CH].rearrange("p (n c) -> p n c", c=CH)
            nc.vector.tensor_tensor(out=sv[:, :, 0:K], in0=ex[:], in1=rs[:].unsqueeze(2).to_broadcast([P, H, K]), op=ALU.mult)

        def sp_write(t):
            if not ok(t):
                return
            nc.sync.dma_start(out=flat[t * 131072:(t + 1) * 131072].rearrange("(p w) -> p w", w=1024), in_=stages[t % 3][:])

        def sp_reads(t):
            if not ok(t):
                return
            bt = bands[t % NBAND]
            ct = corners[t % NBAND]
            for a in range(4):
                base = t * 131072 + a * 32 * 1024
                src = flat[base:base + 32 * 1023].rearrange("(i w) -> i w", w=1023)[:, 0:H * CH].rearrange("i (n c) -> i n c", c=CH)
                if a == 0:
                    if t >= NB:
                        for j in range(4):
                            nc.sync.dma_start(out=ct[32 * j:32 * j + 32, :, 32 * j + 1:32 * j + 32], in_=src[:, 4 * j:4 * j + 4, 0:31])
                    nc.sync.dma_start(out=bt[0:32, :, 0:32], in_=src[:, :, 31:63])
                else:
                    nc.sync.dma_start(out=bt[32 * a:32 * a + 32, :, 32 * (a - 1) + 1:32 * (a - 1) + 64], in_=src[:, :, 0:63])

        def dve_lc(t):
            if not ok(t) or t < NB:
                return
            lc = p2.tile([P, 4, P], F32, name="lc", tag="lc", align_bytes=64)
            nc.vector.transpose(out=lc[:].rearrange("p q c -> p (q c)"), in_=corners[t % NBAND][:].rearrange("p q c -> p (q c)"))
            T[("lc", t)] = lc

        def pool_hcf(t):
            if not ok(t) or t < NB:
                return
            hcf = p2.tile([P, 256], F32, name="hcf", tag="hcf")
            nc.scalar.copy(out=hcf[:], in_=T[("hcb", t // NB)][:, t % NB, :])
            T[("hcf", t)] = hcf

        def pe_cornermm(t):
            if not ok(t) or t < NB:
                return
            yk = ps_t.tile([P, 256], F32, name="yk", tag="tp")
            lc = T[("lc", t)]
            hcf = T[("hcf", t)]
            for q in range(4):
                nc.tensor.matmul(out=yk[:, R * q:R * q + R], lhsT=lc[:, q, :], rhs=hcf[:, R * q:R * q + R], start=True, stop=True)
            T[("yk", t)] = yk

        def act_ysb(t):
            if not ok(t) or t < NB:
                return
            ysb = p2.tile([P, 256], F32, name="ysb", tag="ysb")
            nc.scalar.copy(out=ysb[:], in_=T[("yk", t)][:])
            T[("ysb", t)] = ysb

        def pe_bandT(t, j):
            if not ok(t):
                return
            off = (P - 32 * j) % P
            tp = ps_t.tile([P, 4, P], F32, name="tp", tag="tp")
            for q in range(4):
                nc.tensor.transpose(tp[:, q, :], bands[t % NBAND][:, 4 * j + q, :], idf[:, off:off + P])
            T[("ltT", t, j)] = tp

        def act_lt(t, j):
            if not ok(t):
                return
            if j == 0:
                T[("lt", t)] = p2.tile([P, H, P], F32, name="lt", tag="lt")
            nc.scalar.copy(out=T[("lt", t)][:, 4 * j:4 * j + 4, :], in_=T[("ltT", t, j)][:])

        def pe_mm(t, j):
            if not ok(t):
                return
            if j % 2 == 0:
                T[("cd", t, j // 2)] = ps_c.tile([P, 512], F32, name="cd", tag="cd")
            cd = T[("cd", t, j // 2)]
            lt = T[("lt", t)]
            hf = T[("hf", t)]
            for q in range(4):
                n = 4 * j + q
                m = n % 8
                nc.tensor.matmul(out=cd[:, R * m:R * m + R], lhsT=lt[:, n, :], rhs=hf[:, R * n:R * n + R], start=True, stop=True)

        def dve_c(t, half):
            if not ok(t):
                return
            if half == 0:
                T[("cb", t)] = p2.tile([P, C], BF16, name="cb", tag="cb")
            cb = T[("cb", t)]
            cd = T[("cd", t, half)]
            if t < NB:
                nc.vector.tensor_copy(out=cb[:, 512 * half:512 * half + 512], in_=cd[:])
            else:
                for j in (2 * half, 2 * half + 1):
                    nc.vector.scalar_tensor_tensor(out=cb[:, 256 * j:256 * j + 256], in0=T[("ysb", t)][:], scalar=msk[:, j:j + 1],
                                                   in1=cd[:, 256 * (j % 2):256 * (j % 2) + 256], op0=ALU.mult, op1=ALU.add)

        def pe_cT(t):
            if not ok(t):
                return
            tpb = ps_t.tile([P, 8, P], BF16, name="tpb", tag="tp")
            cb = T[("cb", t)]
            for ch in range(8):
                j = ch // 2
                nc.tensor.transpose(tpb[:, ch, :], cb[:, P * ch:P * ch + P], idb[:, 32 * j:32 * j + P])
            T[("cT", t)] = tpb

        def act_cg(t):
            if not ok(t):
                return
            cg = p2.tile([P, C], BF16, name="cg", tag="cg", align_bytes=64)
            nc.scalar.copy(out=cg[:].rearrange("p (g r t) -> p g r t", g=2, t=4), in_=T[("cT", t)][:].rearrange("p (g t) r -> p g r t", g=2))
            T[("cg", t)] = cg

        def dve_qc(t):
            if not ok(t):
                return
            cq = p2.tile([P, 256], U32, name="cq", tag="cq", align_bytes=64)
            cs = p2.tile([P, 256], U8, name="cs", tag="cs", align_bytes=64)
            nc.vector.quantize_mx(out=cq[:].bitcast(FP8X4), scales=cs[:], in_=T[("cg", t)][:])
            T[("cq", t)] = (cq, cs)

        def pe_mm2(t):
            if not ok(t):
                return
            cq, cs = T[("cq", t)]
            for e2 in range(2):
                yp = ps_y.tile([P, 512], F32, name="yp", tag="yp")
                for g in range(2):
                    nc.tensor.matmul_mx(out=yp[:], lhsT=cq[:, P * g:P * g + P].bitcast(FP8X4), lhsT_scale=cs[:, P * g:P * g + P],
                                        rhs=w2q[:, g, 512 * e2:512 * e2 + 512].bitcast(FP8X4), rhs_scale=w2s[:, g, 512 * e2:512 * e2 + 512],
                                        start=(g == 0), stop=(g == 1))
                T[("yp", t, e2)] = yp

        def pool_xb(t):
            if not ok(t):
                return
            xb = p3.tile([P, C], F32, name="xb", tag="xb")
            nc.vector.tensor_tensor(out=xb[:], in0=T[("xt", t)][:], in1=b2_bc[:], op=ALU.add)
            T[("xb", t)] = xb

        def dve_v(t):
            if not ok(t):
                return
            v = p2.tile([P, C], F32, name="v", tag="v")
            s2 = p2.tile([P, 2], F32, name="s2", tag="s2")
            xb = T[("xb", t)]
            for e2 in range(2):
                nc.vector.scalar_tensor_tensor(out=v[:, 512 * e2:512 * e2 + 512], in0=T[("yp", t, e2)][:], scalar=1.0,
                                               in1=xb[:, 512 * e2:512 * e2 + 512], op0=ALU.mult, op1=ALU.add, accum_out=s2[:, e2:e2 + 1])
            nm = p2.tile([P, 1], F32, name="nm", tag="nm")
            nc.vector.tensor_scalar(out=nm[:], in0=s2[:, 0:1], scalar1=s2[:, 1:2], scalar2=-1.0 / C, op0=ALU.add, op1=ALU.mult)
            T[("v", t)] = v
            T[("nm", t)] = nm

        def act_sq(t):
            if not ok(t):
                return
            junk = p1.tile([P, C], BF16, name="junk", tag="junk")
            ss = p2.tile([P, 1], F32, name="ss", tag="ss")
            nc.scalar.activation(out=junk[:], in_=T[("v", t)][:], func=ACT.Square, bias=T[("nm", t)][:], scale=1.0, accum_out=ss[:])
            T[("ss", t)] = ss

        def pool_rstd(t):
            if not ok(t):
                return
            ve = p2.tile([P, 1], F32, name="ve", tag="ve")
            nc.gpsimd.tensor_scalar(out=ve[:], in0=T[("ss", t)][:], scalar1=1.0 / C, scalar2=EPS, op0=ALU.mult, op1=ALU.add)
            rstd = p2.tile([P, 1], F32, name="rstd", tag="rstd")
            nc.gpsimd.tensor_tensor(out=rstd[:], in0=ve[:], in1=nhalf[:], op=ALU.pow)
            T[("rstd", t)] = rstd

        def dve_A(t):
            if not ok(t):
                return
            t1 = p2.tile([P, C], F32, name="t1", tag="t1")
            nc.vector.scalar_tensor_tensor(out=t1[:], in0=T[("v", t)][:], scalar=T[("nm", t)][:], in1=g_bc[:], op0=ALU.add, op1=ALU.mult)
            T[("t1", t)] = t1

        def dve_B(t):
            if not ok(t):
                return
            t1 = T[("t1", t)]
            nc.vector.scalar_tensor_tensor(out=t1[:], in0=t1[:], scalar=T[("rstd", t)][:], in1=be_bc[:], op0=ALU.mult, op1=ALU.add)

        def sp_store(t):
            if not ok(t):
                return
            nc.sync.dma_start(out=out[P * (t // NB):P * (t // NB) + P, t % NB, :], in_=T[("t1", t)][:])

        def w2_load(rt):
            raw = wst.tile([P, C], BF16, name="raw", tag="raw")
            nc.sync.dma_start(out=raw[:], in_=w2[P * rt:P * rt + P, :])
            T[("raw", rt)] = raw

        def w2_prep(rt):
            tpb = ps_t.tile([P, 8, P], BF16, name="tpb", tag="tp")
            raw = T[("raw", rt)]
            for gt in range(8):
                nc.tensor.transpose(tpb[:, gt, :], raw[:, P * gt:P * gt + P], idb[:, 0:P])
            nc.scalar.copy(out=gw2v[:, :, P * rt:P * rt + P, :], in_=tpb[:].rearrange("p (g t) r -> p g r t", g=2))

        for s in range(NT + 8):
            ld(s + 1)
            if 1 - 1 <= s < 1 + 3:
                w2_load(2 * (s - 1 + 1))
                w2_load(2 * (s - 1 + 1) + 1)
            if s == 1:
                nc.sync.dma_start(out=b2_bc[:], in_=b2.partition_broadcast(P))
            if s == 2:
                nc.sync.dma_start(out=g_bc[:], in_=gamma.partition_broadcast(P))
                nc.sync.dma_start(out=be_bc[:], in_=beta.partition_broadcast(P))
            ld_x(s - 3)
            if (s - 3) % NB == 0 and NB <= s - 3 < NT:
                ld_hc((s - 3) // NB)
            sp_reads(s - 3)

            pe_mm(s - 5, 0)
            pe_cT(s - 6)
            dve_v(s - 7)
            act_cg(s - 6)
            pe_mm(s - 5, 1)
            pe_hT(s)
            act_hg(s)
            dve_sm1(s - 2)
            dve_qc(s - 6)
            pe_cornermm(s - 5)
            act_ysb(s - 5)
            act_sq(s - 7)
            pe_bandT(s - 4, 0)
            act_lt(s - 4, 0)
            dve_A(s - 7)
            pool_xb(s - 5)
            pe_bandT(s - 4, 1)
            act_lt(s - 4, 1)
            act_exp(s - 2)
            dve_c(s - 5, 0)
            dve_qh(s)
            dve_lc(s - 4)
            pool_rstd(s - 7)
            pe_mm(s - 5, 2)
            dve_sm2(s - 2)
            sp_write(s - 2)
            pe_bandT(s - 4, 2)
            act_lt(s - 4, 2)
            pe_bandT(s - 4, 3)
            act_lt(s - 4, 3)
            pe_mm(s - 5, 3)
            dve_B(s - 7)
            sp_store(s - 7)
            pool_hf(s)
            pool_hcf(s - 4)
            pe_mm1(s - 1)
            pe_mm2(s - 6)
            dve_c(s - 5, 1)
            if 1 <= s < 1 + 4:
                w2_prep(2 * (s - 1))
                w2_prep(2 * (s - 1) + 1)
            if 2 <= s < 4:
                nc.vector.memset(bands[s - 1][:], 0.0)
            if s == 4:
                for ct in corners:
                    nc.vector.memset(ct[:], 0.0)
            if s == 1 + 4:
                for g in range(2):
                    nc.vector.quantize_mx(out=w2q[:, g, :].bitcast(FP8X4), scales=w2s[:, g, :], in_=gw2[:, 4096 * g:4096 * g + 4096])
